import numpy as np
import ml_dtypes


def mxq(x, axis, fmt="e4m3"):
    dtype, down = {"e4m3": (ml_dtypes.float8_e4m3fn, 7), "e5m2": (ml_dtypes.float8_e5m2, 14)}[fmt]
    v = np.moveaxis(np.asarray(x, np.float32).astype(ml_dtypes.bfloat16).astype(np.float64), axis, -1)
    blocks = v.reshape(v.shape[:-1] + (-1, 32))
    amax = np.abs(blocks).max(-1, keepdims=True)
    byte = np.maximum(np.where(amax > 0, np.frexp(amax)[1] - 1 + 127, 0) - down, 1)
    scale = np.exp2(byte - 127.0)
    codes = (blocks / scale).astype(np.float32).astype(dtype).astype(np.float64)
    return np.moveaxis((codes * scale).reshape(v.shape), -1, axis)


WIDE = False


def mx_kscale(k):
    if not WIDE:
        return np.ones(k)
    levels = np.array([10, -10, 5, -5, 0])
    if k % 512:
        return np.exp2(np.random.permutation(np.resize(levels, k // 32))).repeat(32)
    a = np.empty((k // 512, 16))
    for p in range(k // 512):
        a[p, :8] = np.random.permutation(np.resize(levels, 8))
        for g in range(8):
            far = levels[np.abs(levels - a[p, g]) >= 10]
            a[p, g + 8] = far[np.random.randint(len(far))]
    return np.exp2(a.ravel()).repeat(32)


BF16 = ml_dtypes.bfloat16


def bf(x):
    return np.asarray(x, np.float32).astype(BF16)


def f64(x):
    return np.asarray(x).astype(np.float64)


B, L, DIMIN, WIDTH, N_HEADS, N_EMBDS = 8, 128, 512, 2048, 8, 64
EPS = 1e-6
XS = 10.0
SD = np.sqrt(DIMIN / WIDTH)


def setup_inputs():
    s = mx_kscale(WIDTH)
    t = mx_kscale(WIDTH)
    return {"o": bf(np.random.standard_normal((B, L, WIDTH)) * 0.6 * s),
            "o_w": bf(np.random.standard_normal((WIDTH, WIDTH)) * 0.5 / np.sqrt(WIDTH) / s[None, :] * t[:, None]),
            "o_b": bf(np.random.standard_normal(WIDTH) * 0.1 * t),
            "D": bf(np.random.standard_normal((WIDTH, DIMIN)) * SD / t[:, None]),
            "x": bf(np.random.standard_normal((B, L, DIMIN)) * XS)}


def reference(o, o_w, o_b, D, x):
    xc = f64(x)
    d_target = (mxq(f64(o), 2, "e4m3") @ mxq(f64(o_w), 1, "e4m3").T) + f64(o_b)
    z_pred_ = np.maximum(d_target, 0.0)
    Dz = mxq(z_pred_, 2, "e4m3") @ mxq(f64(D), 0, "e4m3")
    Dz_norm = np.sqrt(np.sum(Dz * Dz, axis=-1, keepdims=True)) + EPS
    proj_scale = np.sum(Dz * xc, axis=-1, keepdims=True) / np.square(Dz_norm)
    z_pred = z_pred_ * proj_scale
    x_pred = proj_scale * Dz
    return z_pred, x_pred

@@ -1,0 +1,277 @@
+from contextlib import ExitStack
+
+import concourse.mybir as mybir
+from concourse.masks import make_identity
+
+F32 = mybir.dt.float32
+BF16 = mybir.dt.bfloat16
+U32 = mybir.dt.uint32
+U8 = mybir.dt.uint8
+FP8X4 = mybir.dt.float8_e4m3fn_x4
+ACT = mybir.ActivationFunctionType
+ALU = mybir.AluOpType
+
+P = 128
+PACK = 4
+K_PASS = P * PACK
+ROWS = 1024
+WIDTH = 2048
+DIM = 512
+PASSES = WIDTH // K_PASS
+GROUPS = WIDTH // K_PASS
+PAIR = 2 * P
+W_PAIRS = WIDTH // PAIR
+EPS = 1e-6
+RAW_BUFS = 4
+RUN = 4
+CHUNKS = ((0, 512), (512, 256), (768, 256))
+FIRST_POST = 2
+
+FLOPS = 2 * ROWS * WIDTH * WIDTH + 2 * ROWS * WIDTH * DIM
+
+
+def tile_originaltemporalsae_pa_kernel(tc, o, o_w, o_b, D, x, out_0, out_1):
+    nc = tc.nc
+    o_rows = o.flatten_outer_dims()
+    x_rows = x.flatten_outer_dims()
+    z_rows = out_0.flatten_outer_dims()
+    xp_rows = out_1.flatten_outer_dims()
+
+    views = {}
+    for a in range(ROWS // PAIR):
+        views[("o", a)] = o_rows.rearrange("(a t p) k -> a p t k", t=2, p=P)[a]
+    for a in range(W_PAIRS):
+        views[("w", a)] = o_w.rearrange("(a p h t) k -> a h p t k", p=P, h=2, t=2)[a // 2, a % 2]
+    for a in range(GROUPS // 2):
+        views[("D", a)] = D.rearrange("(a g p j) n -> a p g (j n)", g=2, p=P, j=PACK)[a]
+    load_order = (
+        [("o", 0), ("o", 1)]
+        + [("w", a) for a in range(W_PAIRS)]
+        + [("D", 0), ("D", 1), ("o", 2), ("o", 3)]
+    )
+
+    with ExitStack() as ctx:
+        const = ctx.enter_context(tc.tile_pool(name="const", bufs=1))
+        raw_pool = ctx.enter_context(tc.tile_pool(name="raw", bufs=RAW_BUFS))
+        stage = ctx.enter_context(tc.tile_pool(name="stage", bufs=2))
+        relu_pool = ctx.enter_context(tc.tile_pool(name="relu", bufs=GROUPS))
+        out_pool = ctx.enter_context(tc.tile_pool(name="outp", bufs=4))
+        psum = ctx.enter_context(tc.psum_pool(name="psum", bufs=2))
+        ctx.enter_context(tc.manual_schedule())
+
+        w_codes = const.tile([P, PASSES, WIDTH], U32, align_bytes=64)
+        w_scales = const.tile([P, PASSES, WIDTH], U8, align_bytes=64)
+        o_codes = const.tile([P, PASSES, ROWS], U32, align_bytes=64)
+        o_scales = const.tile([P, PASSES, ROWS], U8, align_bytes=64)
+        d_codes = const.tile([P, GROUPS, DIM], U32, align_bytes=64)
+        d_scales = const.tile([P, GROUPS, DIM], U8, align_bytes=64)
+        x_sb = const.tile([P, ROWS // P, DIM], BF16)
+        ident = const.tile([P, P], F32)
+        bias_raw = const.tile([P, GROUPS, PACK], BF16)
+        bias = const.tile([P, GROUPS * PACK], F32)
+        eps = const.tile([P, 1], F32)
+        warm = const.tile([P, 1], F32)
+        sum_sq = const.tile([P, ROWS // P], F32)
+        norm = const.tile([P, ROWS // P], F32)
+        norm_sq = const.tile([P, ROWS // P], F32)
+        dot = const.tile([P, ROWS // P], F32)
+        inv = const.tile([P, ROWS // P], F32)
+        proj = const.tile([P, ROWS // P], F32)
+
+        raw_tiles = {}
+
+        def load_next():
+            if len(raw_tiles) < len(load_order):
+                key = load_order[len(raw_tiles)]
+                raw = raw_pool.tile([P, 2, WIDTH], BF16, tag="raw")
+                nc.sync.dma_start(out=raw[:], in_=views[key])
+                raw_tiles[key] = raw
+
+        def prepare_pair(key, codes, scales):
+            words = raw_tiles[key][:].bitcast(F32)
+            cols = slice(key[1] * PAIR, (key[1] + 1) * PAIR)
+            grouped = stage.tile([P, PASSES, PAIR, PACK], BF16, tag="grouped", align_bytes=64)
+            grouped_words = grouped[:].bitcast(F32)
+            for c in range(PASSES):
+                bank = psum.tile([P, 2, PAIR], F32, tag="tp", bufs=4)
+                for u in range(2):
+                    for t in range(2):
+                        nc.tensor.transpose(
+                            bank[:, u, t * P : (t + 1) * P],
+                            words[:, t, 2 * c * P + u : 2 * (c + 1) * P : 2],
+                            ident[:],
+                        )
+                turned = bank[:].rearrange("q u m -> q m u")
+                if c < PASSES - 1:
+                    nc.scalar.copy(out=grouped_words[:, c], in_=turned)
+                else:
+                    nc.vector.tensor_copy(out=grouped_words[:, c], in_=turned)
+            for c in range(PASSES):
+                nc.vector.quantize_mx(
+                    out=codes[:, c, cols].bitcast(FP8X4),
+                    scales=scales[:, c, cols],
+                    in_=grouped[:, c].rearrange("q m t -> q (m t)"),
+                )
+
+        def prepare_d(g):
+            raw = raw_tiles[("D", g // 2)]
+            grouped_d = stage.tile([P, DIM, PACK], BF16, tag="grouped_k", align_bytes=64)
+            nc.vector.tensor_copy(
+                out=grouped_d[:].rearrange("p (c i) j -> p c j i", i=RUN),
+                in_=raw[:, g % 2].rearrange("p (j c i) -> p c j i", j=PACK, i=RUN),
+            )
+            nc.vector.quantize_mx(
+                out=d_codes[:, g].bitcast(FP8X4),
+                scales=d_scales[:, g],
+                in_=grouped_d[:].rearrange("p n j -> p (n j)"),
+            )
+
+        relu_t = {}
+        r_codes = {}
+        r_scales = {}
+
+        def stage1_pair(n, a):
+            row0, rows = CHUNKS[n]
+            g = a // 2
+            if a % 2 == 0:
+                r_tile = relu_pool.tile([P, PACK, rows], F32, tag="relu%d" % (n % 2))
+                relu_t[(n, g)] = r_tile
+            for t in range(2):
+                m = 2 * a + t
+                acc = psum.tile([P, rows], F32, tag="acc")
+                for c in range(PASSES):
+                    nc.tensor.matmul_mx(
+                        out=acc[:],
+                        lhsT=w_codes[:, c, m * P : (m + 1) * P].bitcast(FP8X4),
+                        lhsT_scale=w_scales[:, c, m * P : (m + 1) * P],
+                        rhs=o_codes[:, c, row0 : row0 + rows].bitcast(FP8X4),
+                        rhs_scale=o_scales[:, c, row0 : row0 + rows],
+                        start=(c == 0),
+                        stop=(c == PASSES - 1),
+                    )
+                nc.scalar.activation(
+                    out=relu_t[(n, g)][:, m % PACK],
+                    in_=acc[:],
+                    func=ACT.Relu,
+                    bias=bias[:, m : m + 1],
+                    scale=1.0,
+                )
+
+        def quantise_r(n, g):
+            rows = CHUNKS[n][1]
+            if g == 0:
+                codes = const.tile([P, GROUPS, rows], U32, tag="r_codes%d" % (n % 2), align_bytes=64)
+                scales = const.tile([P, GROUPS, rows], U8, tag="r_scales%d" % (n % 2), align_bytes=64)
+                r_codes[n] = codes
+                r_scales[n] = scales
+            grouped_r = stage.tile([P, rows, PACK], BF16, tag="grouped_k", align_bytes=64)
+            nc.vector.tensor_copy(
+                out=grouped_r[:].rearrange("p (c i) j -> p c j i", i=RUN),
+                in_=relu_t[(n, g)][:].rearrange("p j (c i) -> p c j i", i=RUN),
+            )
+            nc.vector.quantize_mx(
+                out=r_codes[n][:, g].bitcast(FP8X4),
+                scales=r_scales[n][:, g],
+                in_=grouped_r[:].rearrange("p r j -> p (r j)"),
+            )
+
+        def stage2_tile(n, local):
+            i = CHUNKS[n][0] // P + local
+            here = slice(local * P, (local + 1) * P)
+            one = slice(i, i + 1)
+            dz = psum.tile([P, DIM], F32, tag="dz")
+            for g in range(GROUPS):
+                nc.tensor.matmul_mx(
+                    out=dz[:],
+                    lhsT=r_codes[n][:, g, here].bitcast(FP8X4),
+                    lhsT_scale=r_scales[n][:, g, here],
+                    rhs=d_codes[:, g].bitcast(FP8X4),
+                    rhs_scale=d_scales[:, g],
+                    start=(g == 0),
+                    stop=(g == GROUPS - 1),
+                )
+            squares = stage.tile([P, DIM], F32, tag="squares")
+            nc.scalar.activation(out=squares[:], in_=dz[:], func=ACT.Square, accum_out=sum_sq[:, one])
+            products = stage.tile([P, DIM], F32, tag="products")
+            nc.vector.scalar_tensor_tensor(
+                out=products[:],
+                in0=dz[:],
+                scalar=1.0,
+                in1=x_sb[:, i],
+                op0=ALU.mult,
+                op1=ALU.mult,
+                accum_out=dot[:, one],
+            )
+            nc.scalar.activation(out=norm[:, one], in_=sum_sq[:, one], func=ACT.Sqrt)
+            nc.scalar.activation(out=norm_sq[:, one], in_=norm[:, one], func=ACT.Square, bias=eps[:, 0:1])
+            nc.vector.reciprocal(out=inv[:, one], in_=norm_sq[:, one])
+            nc.vector.tensor_tensor(out=proj[:, one], in0=dot[:, one], in1=inv[:, one], op=ALU.mult)
+            x_pred = out_pool.tile([P, DIM], F32, tag="x_pred", bufs=2)
+            nc.scalar.activation(out=x_pred[:], in_=dz[:], func=ACT.Copy, scale=proj[:, one])
+            nc.sync.dma_start(out=xp_rows[i * P : (i + 1) * P, :], in_=x_pred[:])
+
+        def z_tile(n, local):
+            i = CHUNKS[n][0] // P + local
+            here = slice(local * P, (local + 1) * P)
+            one = slice(i, i + 1)
+            for half in range(GROUPS // 2):
+                z_sb = out_pool.tile([P, 2, P, PACK], F32, tag="z_sb")
+                for s in range(2):
+                    g = 2 * half + s
+                    bank = psum.tile([P, PACK, P], F32, tag="tp", bufs=4)
+                    for j in range(PACK):
+                        nc.tensor.transpose(bank[:, j], relu_t[(n, g)][:, j, here], ident[:])
+                    turned = bank[:].rearrange("r j p -> r p j")
+                    if s == 0:
+                        nc.scalar.activation(out=z_sb[:, s], in_=turned, func=ACT.Copy, scale=proj[:, one])
+                    else:
+                        nc.vector.tensor_scalar(
+                            out=z_sb[:, s], in0=turned, scalar1=proj[:, one], scalar2=None, op0=ALU.mult
+                        )
+                nc.sync.dma_start(
+                    out=z_rows[i * P : (i + 1) * P, half * 2 * K_PASS : (half + 1) * 2 * K_PASS],
+                    in_=z_sb[:].rearrange("r s p j -> r (s p j)"),
+                )
+
+        for k in range(RAW_BUFS):
+            load_next()
+        nc.scalar.dma_start(out=bias_raw[:], in_=o_b.rearrange("(g p j) -> p g j", p=P, j=PACK))
+        make_identity(nc, ident[:])
+        nc.vector.memset(eps[:], EPS)
+        nc.scalar.activation(out=warm[:], in_=eps[:], func=ACT.Sqrt)
+        nc.vector.tensor_copy(out=bias[:], in_=bias_raw[:].rearrange("p g j -> p (g j)"))
+
+        steps = [("o", 0), ("o", 1)] + [("w", a) for a in range(W_PAIRS)] + [("o", 2), ("o", 3)]
+        for k, key in enumerate(steps):
+            if key[0] == "o":
+                prepare_pair(key, o_codes, o_scales)
+            else:
+                prepare_pair(key, w_codes, w_scales)
+            load_next()
+            before = steps[k - 1] if k > 0 else ("o", 0)
+            before2 = steps[k - 2] if k > 1 else ("o", 0)
+            if before2[0] == "w" and before2[1] % 2 == 1:
+                quantise_r(0, before2[1] // 2)
+            if k >= len(steps) - GROUPS:
+                prepare_d(k - (len(steps) - GROUPS))
+            if before[0] == "w":
+                stage1_pair(0, before[1])
+        nc.sync.dma_start(out=x_sb[:], in_=x_rows.rearrange("(t p) n -> p t n", p=P))
+
+        for n in range(1, len(CHUNKS)):
+            tiles_before = CHUNKS[n - 1][1] // P
+            for a in range(W_PAIRS):
+                stage1_pair(n, a)
+                if a % 2 == 0 and a > 0:
+                    quantise_r(n, a // 2 - 1)
+                if 0 <= a - FIRST_POST < tiles_before:
+                    stage2_tile(n - 1, a - FIRST_POST)
+                if 0 <= a - FIRST_POST - 2 < tiles_before:
+                    z_tile(n - 1, a - FIRST_POST - 2)
+            quantise_r(n, GROUPS - 1)
+
+        last = len(CHUNKS) - 1
+        for local in range(CHUNKS[last][1] // P):
+            stage2_tile(last, local)
+        for local in range(CHUNKS[last][1] // P):
+            z_tile(last, local)

@@ -15,6 +15,7 @@ P = 128
 PACK = 4
 K_PASS = P * PACK
 ROWS = 1024
+TILES = ROWS // P
 WIDTH = 2048
 DIM = 512
 PASSES = WIDTH // K_PASS
@@ -22,10 +23,9 @@ GROUPS = WIDTH // K_PASS
 PAIR = 2 * P
 W_PAIRS = WIDTH // PAIR
 EPS = 1e-6
-RAW_BUFS = 4
+RAW_BUFS = 6
 RUN = 4
-CHUNKS = ((0, 512), (512, 256), (768, 256))
-FIRST_POST = 2
+EARLY = 2
 
 FLOPS = 2 * ROWS * WIDTH * WIDTH + 2 * ROWS * WIDTH * DIM
 
@@ -41,42 +41,42 @@ def tile_originaltemporalsae_pa_kernel(tc, o, o_w, o_b, D, x, out_0, out_1):
     for a in range(ROWS // PAIR):
         views[("o", a)] = o_rows.rearrange("(a t p) k -> a p t k", t=2, p=P)[a]
     for a in range(W_PAIRS):
-        views[("w", a)] = o_w.rearrange("(a p h t) k -> a h p t k", p=P, h=2, t=2)[a // 2, a % 2]
+        views[("w", a)] = o_w.rearrange("(a t p) k -> a p t k", t=2, p=P)[a]
     for a in range(GROUPS // 2):
         views[("D", a)] = D.rearrange("(a g p j) n -> a p g (j n)", g=2, p=P, j=PACK)[a]
     load_order = (
-        [("o", 0), ("o", 1)]
+        [("o", 0)]
         + [("w", a) for a in range(W_PAIRS)]
-        + [("D", 0), ("D", 1), ("o", 2), ("o", 3)]
+        + [("D", 0), ("D", 1), ("o", 1), ("o", 2), ("o", 3)]
     )
 
     with ExitStack() as ctx:
         const = ctx.enter_context(tc.tile_pool(name="const", bufs=1))
         raw_pool = ctx.enter_context(tc.tile_pool(name="raw", bufs=RAW_BUFS))
         stage = ctx.enter_context(tc.tile_pool(name="stage", bufs=2))
-        relu_pool = ctx.enter_context(tc.tile_pool(name="relu", bufs=GROUPS))
-        out_pool = ctx.enter_context(tc.tile_pool(name="outp", bufs=4))
+        d_pool = ctx.enter_context(tc.tile_pool(name="dpool", bufs=4))
         psum = ctx.enter_context(tc.psum_pool(name="psum", bufs=2))
         ctx.enter_context(tc.manual_schedule())
 
         w_codes = const.tile([P, PASSES, WIDTH], U32, align_bytes=64)
         w_scales = const.tile([P, PASSES, WIDTH], U8, align_bytes=64)
-        o_codes = const.tile([P, PASSES, ROWS], U32, align_bytes=64)
-        o_scales = const.tile([P, PASSES, ROWS], U8, align_bytes=64)
+        o_codes = const.tile([P, TILES, PASSES, P], U32, align_bytes=64)
+        o_scales = const.tile([P, TILES, PASSES, P], U8, align_bytes=64)
         d_codes = const.tile([P, GROUPS, DIM], U32, align_bytes=64)
         d_scales = const.tile([P, GROUPS, DIM], U8, align_bytes=64)
-        x_sb = const.tile([P, ROWS // P, DIM], BF16)
+        x_sb = const.tile([P, TILES, DIM], BF16)
         ident = const.tile([P, P], F32)
-        bias_raw = const.tile([P, GROUPS, PACK], BF16)
-        bias = const.tile([P, GROUPS * PACK], F32)
+        bias_row = const.tile([P, WIDTH], BF16)
+        ones = const.tile([P, P], BF16)
+        bias = const.tile([P, WIDTH], F32)
         eps = const.tile([P, 1], F32)
         warm = const.tile([P, 1], F32)
-        sum_sq = const.tile([P, ROWS // P], F32)
-        norm = const.tile([P, ROWS // P], F32)
-        norm_sq = const.tile([P, ROWS // P], F32)
-        dot = const.tile([P, ROWS // P], F32)
-        inv = const.tile([P, ROWS // P], F32)
-        proj = const.tile([P, ROWS // P], F32)
+        sum_sq = const.tile([P, TILES], F32)
+        norm = const.tile([P, TILES], F32)
+        norm_sq = const.tile([P, TILES], F32)
+        dot = const.tile([P, TILES], F32)
+        inv = const.tile([P, TILES], F32)
+        proj = const.tile([P, TILES], F32)
 
         raw_tiles = {}
 
@@ -84,112 +84,150 @@ def tile_originaltemporalsae_pa_kernel(tc, o, o_w, o_b, D, x, out_0, out_1):
             if len(raw_tiles) < len(load_order):
                 key = load_order[len(raw_tiles)]
                 raw = raw_pool.tile([P, 2, WIDTH], BF16, tag="raw")
-                nc.sync.dma_start(out=raw[:], in_=views[key])
+                for t in range(2):
+                    nc.sync.dma_start(out=raw[:, t], in_=views[key][:, t])
                 raw_tiles[key] = raw
 
-        def prepare_pair(key, codes, scales):
+        def copy_out(engine, out, in_):
+            if engine == "S":
+                nc.scalar.copy(out=out, in_=in_)
+            else:
+                nc.vector.tensor_copy(out=out, in_=in_)
+
+        def turn(key, t, h):
             words = raw_tiles[key][:].bitcast(F32)
-            cols = slice(key[1] * PAIR, (key[1] + 1) * PAIR)
-            grouped = stage.tile([P, PASSES, PAIR, PACK], BF16, tag="grouped", align_bytes=64)
-            grouped_words = grouped[:].bitcast(F32)
-            for c in range(PASSES):
-                bank = psum.tile([P, 2, PAIR], F32, tag="tp", bufs=4)
+            bank = psum.tile([P, 2, 2, P], F32, tag="tp", bufs=4)
+            for s in range(2):
                 for u in range(2):
-                    for t in range(2):
-                        nc.tensor.transpose(
-                            bank[:, u, t * P : (t + 1) * P],
-                            words[:, t, 2 * c * P + u : 2 * (c + 1) * P : 2],
-                            ident[:],
-                        )
-                turned = bank[:].rearrange("q u m -> q m u")
-                if c < PASSES - 1:
-                    nc.scalar.copy(out=grouped_words[:, c], in_=turned)
-                else:
-                    nc.vector.tensor_copy(out=grouped_words[:, c], in_=turned)
+                    c = 2 * h + s
+                    nc.tensor.transpose(
+                        bank[:, s, u], words[:, t, 2 * c * P + u : 2 * (c + 1) * P : 2], ident[:]
+                    )
+            return bank[:].rearrange("q s u m -> q s m u")
+
+        def prepare_o(i, h, engine):
+            turned = turn(("o", i // 2), i % 2, h)
+            grouped = stage.tile([P, 2, P, PACK], BF16, tag="grouped_o", align_bytes=64, bufs=3)
+            copy_out(engine, grouped[:].bitcast(F32), turned)
+
+            def quantise():
+                nc.vector.quantize_mx(
+                    out=o_codes[:, i, 2 * h : 2 * h + 2].rearrange("p c m -> p (c m)").bitcast(FP8X4),
+                    scales=o_scales[:, i, 2 * h : 2 * h + 2].rearrange("p c m -> p (c m)"),
+                    in_=grouped[:].rearrange("q c m t -> q (c m t)"),
+                )
+
+            return quantise
+
+        def prepare_w(a, engines):
+            grouped = stage.tile([P, PASSES, PAIR, PACK], BF16, tag="grouped_w", align_bytes=64)
+            words = grouped[:].bitcast(F32)
+            for h in range(2):
+                for t in range(2):
+                    turned = turn(("w", a), t, h)
+                    copy_out(engines[2 * h + t], words[:, 2 * h : 2 * h + 2, t * P : (t + 1) * P], turned)
+            cols = slice(a * PAIR, (a + 1) * PAIR)
             for c in range(PASSES):
                 nc.vector.quantize_mx(
-                    out=codes[:, c, cols].bitcast(FP8X4),
-                    scales=scales[:, c, cols],
+                    out=w_codes[:, c, cols].bitcast(FP8X4),
+                    scales=w_scales[:, c, cols],
                     in_=grouped[:, c].rearrange("q m t -> q (m t)"),
                 )
 
-        def prepare_d(g):
+        grouped_d = {}
+
+        def regroup_d(g):
             raw = raw_tiles[("D", g // 2)]
-            grouped_d = stage.tile([P, DIM, PACK], BF16, tag="grouped_k", align_bytes=64)
+            grouped = stage.tile([P, DIM, PACK], BF16, tag="grouped_d", align_bytes=64)
             nc.vector.tensor_copy(
-                out=grouped_d[:].rearrange("p (c i) j -> p c j i", i=RUN),
+                out=grouped[:].rearrange("p (c i) j -> p c j i", i=RUN),
                 in_=raw[:, g % 2].rearrange("p (j c i) -> p c j i", j=PACK, i=RUN),
             )
+            grouped_d[g] = grouped
+
+        def quantise_d(g):
             nc.vector.quantize_mx(
                 out=d_codes[:, g].bitcast(FP8X4),
                 scales=d_scales[:, g],
-                in_=grouped_d[:].rearrange("p n j -> p (n j)"),
+                in_=grouped_d[g][:].rearrange("p n j -> p (n j)"),
             )
 
-        relu_t = {}
+        d_tiles = {}
+        r_tiles = {}
         r_codes = {}
         r_scales = {}
 
-        def stage1_pair(n, a):
-            row0, rows = CHUNKS[n]
-            g = a // 2
-            if a % 2 == 0:
-                r_tile = relu_pool.tile([P, PACK, rows], F32, tag="relu%d" % (n % 2))
-                relu_t[(n, g)] = r_tile
-            for t in range(2):
-                m = 2 * a + t
-                acc = psum.tile([P, rows], F32, tag="acc")
-                for c in range(PASSES):
-                    nc.tensor.matmul_mx(
-                        out=acc[:],
-                        lhsT=w_codes[:, c, m * P : (m + 1) * P].bitcast(FP8X4),
-                        lhsT_scale=w_scales[:, c, m * P : (m + 1) * P],
-                        rhs=o_codes[:, c, row0 : row0 + rows].bitcast(FP8X4),
-                        rhs_scale=o_scales[:, c, row0 : row0 + rows],
-                        start=(c == 0),
-                        stop=(c == PASSES - 1),
-                    )
-                nc.scalar.activation(
-                    out=relu_t[(n, g)][:, m % PACK],
-                    in_=acc[:],
-                    func=ACT.Relu,
-                    bias=bias[:, m : m + 1],
-                    scale=1.0,
+        def stage1(i, g):
+            if g == 0:
+                d_tile = d_pool.tile([P, WIDTH], F32, tag="d")
+                d_tiles[i] = d_tile
+                r_tile = stage.tile([P, GROUPS, 2, P, 2], BF16, tag="r_bf", bufs=3)
+                r_tiles[i] = r_tile
+            cols = slice(g * K_PASS, (g + 1) * K_PASS)
+            acc = psum.tile([P, K_PASS], F32, tag="acc")
+            for c in range(PASSES):
+                nc.tensor.matmul_mx(
+                    out=acc[:],
+                    lhsT=o_codes[:, i, c].bitcast(FP8X4),
+                    lhsT_scale=o_scales[:, i, c],
+                    rhs=w_codes[:, c, cols].bitcast(FP8X4),
+                    rhs_scale=w_scales[:, c, cols],
+                    start=(c == 0),
+                    stop=(c == PASSES - 1),
+                )
+            nc.vector.tensor_tensor(out=d_tiles[i][:, cols], in0=acc[:], in1=bias[:, cols], op=ALU.add)
+
+        def relu(i, g):
+            cols = slice(g * K_PASS, (g + 1) * K_PASS)
+            nc.scalar.activation(
+                out=r_tiles[i][:, g],
+                in_=d_tiles[i][:, cols].rearrange("r (w u e) -> r u w e", u=2, e=2),
+                func=ACT.Relu,
+            )
+
+        def turn_r(i, h, engine):
+            words = r_tiles[i][:].rearrange("r g u w e -> r (g u w e)").bitcast(F32)
+            bank = psum.tile([P, 2, 2, P], F32, tag="tp", bufs=4)
+            for s in range(2):
+                for u in range(2):
+                    first = ((2 * h + s) * 2 + u) * P
+                    nc.tensor.transpose(bank[:, s, u], words[:, first : first + P], ident[:])
+            grouped = stage.tile([P, 2, P, PACK], BF16, tag="grouped_r", align_bytes=64)
+            copy_out(engine, grouped[:].bitcast(F32), bank[:].rearrange("q s u m -> q s m u"))
+            if h == 0:
+                codes = stage.tile([P, GROUPS, P], U32, tag="r_codes", align_bytes=64)
+                scales = stage.tile([P, GROUPS, P], U8, tag="r_scales", align_bytes=64)
+                r_codes[i] = codes
+                r_scales[i] = scales
+
+            def quantise():
+                nc.vector.quantize_mx(
+                    out=r_codes[i][:, 2 * h : 2 * h + 2].rearrange("p g m -> p (g m)").bitcast(FP8X4),
+                    scales=r_scales[i][:, 2 * h : 2 * h + 2].rearrange("p g m -> p (g m)"),
+                    in_=grouped[:].rearrange("q g m t -> q (g m t)"),
                 )
 
-        def quantise_r(n, g):
-            rows = CHUNKS[n][1]
-            if g == 0:
-                codes = const.tile([P, GROUPS, rows], U32, tag="r_codes%d" % (n % 2), align_bytes=64)
-                scales = const.tile([P, GROUPS, rows], U8, tag="r_scales%d" % (n % 2), align_bytes=64)
-                r_codes[n] = codes
-                r_scales[n] = scales
-            grouped_r = stage.tile([P, rows, PACK], BF16, tag="grouped_k", align_bytes=64)
-            nc.vector.tensor_copy(
-                out=grouped_r[:].rearrange("p (c i) j -> p c j i", i=RUN),
-                in_=relu_t[(n, g)][:].rearrange("p j (c i) -> p c j i", i=RUN),
-            )
-            nc.vector.quantize_mx(
-                out=r_codes[n][:, g].bitcast(FP8X4),
-                scales=r_scales[n][:, g],
-                in_=grouped_r[:].rearrange("p r j -> p (r j)"),
-            )
+            return quantise
 
-        def stage2_tile(n, local):
-            i = CHUNKS[n][0] // P + local
-            here = slice(local * P, (local + 1) * P)
-            one = slice(i, i + 1)
+        dz_tiles = {}
+
+        def stage2(i):
             dz = psum.tile([P, DIM], F32, tag="dz")
+            dz_tiles[i] = dz
             for g in range(GROUPS):
                 nc.tensor.matmul_mx(
                     out=dz[:],
-                    lhsT=r_codes[n][:, g, here].bitcast(FP8X4),
-                    lhsT_scale=r_scales[n][:, g, here],
+                    lhsT=r_codes[i][:, g].bitcast(FP8X4),
+                    lhsT_scale=r_scales[i][:, g],
                     rhs=d_codes[:, g].bitcast(FP8X4),
                     rhs_scale=d_scales[:, g],
                     start=(g == 0),
                     stop=(g == GROUPS - 1),
                 )
+
+        def sums(i):
+            one = slice(i, i + 1)
+            dz = dz_tiles[i]
             squares = stage.tile([P, DIM], F32, tag="squares")
             nc.scalar.activation(out=squares[:], in_=dz[:], func=ACT.Square, accum_out=sum_sq[:, one])
             products = stage.tile([P, DIM], F32, tag="products")
@@ -202,76 +240,115 @@ def tile_originaltemporalsae_pa_kernel(tc, o, o_w, o_b, D, x, out_0, out_1):
                 op1=ALU.mult,
                 accum_out=dot[:, one],
             )
+
+        def norms(i):
+            one = slice(i, i + 1)
             nc.scalar.activation(out=norm[:, one], in_=sum_sq[:, one], func=ACT.Sqrt)
             nc.scalar.activation(out=norm_sq[:, one], in_=norm[:, one], func=ACT.Square, bias=eps[:, 0:1])
+
+        def project(i):
+            one = slice(i, i + 1)
             nc.vector.reciprocal(out=inv[:, one], in_=norm_sq[:, one])
             nc.vector.tensor_tensor(out=proj[:, one], in0=dot[:, one], in1=inv[:, one], op=ALU.mult)
-            x_pred = out_pool.tile([P, DIM], F32, tag="x_pred", bufs=2)
-            nc.scalar.activation(out=x_pred[:], in_=dz[:], func=ACT.Copy, scale=proj[:, one])
-            nc.sync.dma_start(out=xp_rows[i * P : (i + 1) * P, :], in_=x_pred[:])
 
-        def z_tile(n, local):
-            i = CHUNKS[n][0] // P + local
-            here = slice(local * P, (local + 1) * P)
+        def finish(i):
             one = slice(i, i + 1)
-            for half in range(GROUPS // 2):
-                z_sb = out_pool.tile([P, 2, P, PACK], F32, tag="z_sb")
-                for s in range(2):
-                    g = 2 * half + s
-                    bank = psum.tile([P, PACK, P], F32, tag="tp", bufs=4)
-                    for j in range(PACK):
-                        nc.tensor.transpose(bank[:, j], relu_t[(n, g)][:, j, here], ident[:])
-                    turned = bank[:].rearrange("r j p -> r p j")
-                    if s == 0:
-                        nc.scalar.activation(out=z_sb[:, s], in_=turned, func=ACT.Copy, scale=proj[:, one])
-                    else:
-                        nc.vector.tensor_scalar(
-                            out=z_sb[:, s], in0=turned, scalar1=proj[:, one], scalar2=None, op0=ALU.mult
-                        )
-                nc.sync.dma_start(
-                    out=z_rows[i * P : (i + 1) * P, half * 2 * K_PASS : (half + 1) * 2 * K_PASS],
-                    in_=z_sb[:].rearrange("r s p j -> r (s p j)"),
+            rows = slice(i * P, (i + 1) * P)
+            x_pred = stage.tile([P, DIM], F32, tag="x_pred")
+            nc.scalar.activation(out=x_pred[:], in_=dz_tiles[i][:], func=ACT.Copy, scale=proj[:, one])
+            nc.sync.dma_start(out=xp_rows[rows, :], in_=x_pred[:])
+            for h in range(2):
+                cols = slice(h * WIDTH // 2, (h + 1) * WIDTH // 2)
+                nc.vector.tensor_scalar(
+                    out=d_tiles[i][:, cols],
+                    in0=d_tiles[i][:, cols],
+                    scalar1=0.0,
+                    scalar2=proj[:, one],
+                    op0=ALU.max,
+                    op1=ALU.mult,
                 )
+                nc.sync.dma_start(out=z_rows[rows, cols], in_=d_tiles[i][:, cols])
 
-        for k in range(RAW_BUFS):
-            load_next()
-        nc.scalar.dma_start(out=bias_raw[:], in_=o_b.rearrange("(g p j) -> p g j", p=P, j=PACK))
-        make_identity(nc, ident[:])
+        nc.vector.memset(bias_row[:], 0.0)
+        nc.vector.memset(ones[:], 1.0)
         nc.vector.memset(eps[:], EPS)
         nc.scalar.activation(out=warm[:], in_=eps[:], func=ACT.Sqrt)
-        nc.vector.tensor_copy(out=bias[:], in_=bias_raw[:].rearrange("p g j -> p (g j)"))
-
-        steps = [("o", 0), ("o", 1)] + [("w", a) for a in range(W_PAIRS)] + [("o", 2), ("o", 3)]
-        for k, key in enumerate(steps):
-            if key[0] == "o":
-                prepare_pair(key, o_codes, o_scales)
-            else:
-                prepare_pair(key, w_codes, w_scales)
+        load_next()
+        nc.sync.dma_start(out=bias_row[0:1, :], in_=o_b.rearrange("(a k) -> a k", a=1))
+        for k in range(RAW_BUFS - 1):
             load_next()
-            before = steps[k - 1] if k > 0 else ("o", 0)
-            before2 = steps[k - 2] if k > 1 else ("o", 0)
-            if before2[0] == "w" and before2[1] % 2 == 1:
-                quantise_r(0, before2[1] // 2)
-            if k >= len(steps) - GROUPS:
-                prepare_d(k - (len(steps) - GROUPS))
-            if before[0] == "w":
-                stage1_pair(0, before[1])
+        make_identity(nc, ident[:])
+
+        for t in range(EARLY):
+            for h in range(2):
+                prepare_o(t, h, "SV"[h])()
+        load_next()
+        for a in range(W_PAIRS + EARLY):
+            if a < W_PAIRS:
+                prepare_w(a, "SSSV" if a < 5 else "SSSS")
+            else:
+                for h in range(2):
+                    prepare_o(a - W_PAIRS + EARLY, h, "SV"[h])()
+            load_next()
+            if a == 0:
+                for g in range(GROUPS):
+                    cols = slice(g * K_PASS, (g + 1) * K_PASS)
+                    bank = psum.tile([P, K_PASS], F32, tag=("acc", "dz")[g // 2])
+                    nc.tensor.matmul(bank[:], lhsT=ones[:], rhs=bias_row[:, cols], start=True, stop=True)
+                    copy_out("SV"[g % 2], bias[:, cols], bank[:])
+            if a >= 3:
+                relu((a - 1) % 2, (a - 3) // 2)
+            if a in (7, 8):
+                turn_r(a - 7, 0, "S")()
+            if a >= 2:
+                stage1(a % 2, (a - 2) // 2)
+            if 0 <= a - 6 < GROUPS:
+                quantise_d(a - 6)
+            if 0 <= a - 5 < GROUPS:
+                regroup_d(a - 5)
         nc.sync.dma_start(out=x_sb[:], in_=x_rows.rearrange("(t p) n -> p t n", p=P))
+        relu(1, GROUPS - 1)
 
-        for n in range(1, len(CHUNKS)):
-            tiles_before = CHUNKS[n - 1][1] // P
-            for a in range(W_PAIRS):
-                stage1_pair(n, a)
-                if a % 2 == 0 and a > 0:
-                    quantise_r(n, a // 2 - 1)
-                if 0 <= a - FIRST_POST < tiles_before:
-                    stage2_tile(n - 1, a - FIRST_POST)
-                if 0 <= a - FIRST_POST - 2 < tiles_before:
-                    z_tile(n - 1, a - FIRST_POST - 2)
-            quantise_r(n, GROUPS - 1)
+        for i in range(EARLY, TILES):
+            for h in range(2):
+                if i == EARLY:
+                    turned_r = (h, 1)
+                    done = (None, 0)[h]
+                    old = None
+                else:
+                    turned_r = (i - 1, h)
+                    done = (i - 2, None)[h]
+                    old = (i - 3 if i == EARLY + 1 else None, i - 2)[h]
+                ready = []
+                if i + 2 < TILES:
+                    ready.append(prepare_o(i + 2, h, "S"))
+                ready.append(turn_r(turned_r[0], turned_r[1], "S"))
+                if old is not None:
+                    finish(old)
+                if done is not None:
+                    stage2(done)
+                    sums(done)
+                stage1(i, 2 * h)
+                relu(i, 2 * h)
+                for quantise in ready:
+                    quantise()
+                if done is not None:
+                    norms(done)
+                stage1(i, 2 * h + 1)
+                relu(i, 2 * h + 1)
+                if done is not None:
+                    project(done)
 
-        last = len(CHUNKS) - 1
-        for local in range(CHUNKS[last][1] // P):
-            stage2_tile(last, local)
-        for local in range(CHUNKS[last][1] // P):
-            z_tile(last, local)
+        last = TILES - 1
+        turn_r(last, 0, "S")()
+        stage2(last - 1)
+        sums(last - 1)
+        turn_r(last, 1, "V")()
+        norms(last - 1)
+        stage2(last)
+        project(last - 1)
+        sums(last)
+        norms(last)
+        finish(last - 1)
+        project(last)
+        finish(last)

@@ -225,20 +225,22 @@ def tile_originaltemporalsae_pa_kernel(tc, o, o_w, o_b, D, x, out_0, out_1):
                     stop=(g == GROUPS - 1),
                 )
 
-        def sums(i):
-            one = slice(i, i + 1)
-            dz = dz_tiles[i]
-            squares = stage.tile([P, DIM], F32, tag="squares")
-            nc.scalar.activation(out=squares[:], in_=dz[:], func=ACT.Square, accum_out=sum_sq[:, one])
-            products = stage.tile([P, DIM], F32, tag="products")
+        def squares(i):
+            squared = stage.tile([P, DIM], F32, tag="squares")
+            nc.scalar.activation(
+                out=squared[:], in_=dz_tiles[i][:], func=ACT.Square, accum_out=sum_sq[:, i : i + 1]
+            )
+
+        def products(i):
+            product = stage.tile([P, DIM], F32, tag="products")
             nc.vector.scalar_tensor_tensor(
-                out=products[:],
-                in0=dz[:],
+                out=product[:],
+                in0=dz_tiles[i][:],
                 scalar=1.0,
                 in1=x_sb[:, i],
                 op0=ALU.mult,
                 op1=ALU.mult,
-                accum_out=dot[:, one],
+                accum_out=dot[:, i : i + 1],
             )
 
         def norms(i):
@@ -327,13 +329,14 @@ def tile_originaltemporalsae_pa_kernel(tc, o, o_w, o_b, D, x, out_0, out_1):
                     finish(old)
                 if done is not None:
                     stage2(done)
-                    sums(done)
+                    squares(done)
                 stage1(i, 2 * h)
                 relu(i, 2 * h)
+                if done is not None:
+                    products(done)
+                    norms(done)
                 for quantise in ready:
                     quantise()
-                if done is not None:
-                    norms(done)
                 stage1(i, 2 * h + 1)
                 relu(i, 2 * h + 1)
                 if done is not None:
@@ -342,13 +345,15 @@ def tile_originaltemporalsae_pa_kernel(tc, o, o_w, o_b, D, x, out_0, out_1):
         last = TILES - 1
         turn_r(last, 0, "S")()
         stage2(last - 1)
-        sums(last - 1)
+        squares(last - 1)
         turn_r(last, 1, "V")()
+        products(last - 1)
         norms(last - 1)
         stage2(last)
         project(last - 1)
-        sums(last)
-        norms(last)
+        squares(last)
         finish(last - 1)
+        products(last)
+        norms(last)
         project(last)
         finish(last)

@@ -23,9 +23,21 @@ GROUPS = WIDTH // K_PASS
 PAIR = 2 * P
 W_PAIRS = WIDTH // PAIR
 EPS = 1e-6
-RAW_BUFS = 6
+RAW_BUFS = 4
 RUN = 4
-EARLY = 2
+EARLY = 4
+SORT_W = ("V", "V")
+SORT_O = "V"
+COPY_T = ("S", "S")
+FIRST_SORT = 6
+LEAD = 2
+R_LAG = 3
+S2_FIRST = 1
+S2_G = 0
+D_FIRST = 18
+D_STEP = 2
+SORT_SET = (0, 1, 2, 3)
+D_LOAD = 10
 
 FLOPS = 2 * ROWS * WIDTH * WIDTH + 2 * ROWS * WIDTH * DIM
 
@@ -44,17 +56,49 @@ def tile_originaltemporalsae_pa_kernel(tc, o, o_w, o_b, D, x, out_0, out_1):
         views[("w", a)] = o_w.rearrange("(a t p) k -> a p t k", t=2, p=P)[a]
     for a in range(GROUPS // 2):
         views[("D", a)] = D.rearrange("(a g p j) n -> a p g (j n)", g=2, p=P, j=PACK)[a]
-    load_order = (
-        [("o", 0)]
-        + [("w", a) for a in range(W_PAIRS)]
-        + [("D", 0), ("D", 1), ("o", 1), ("o", 2), ("o", 3)]
-    )
+
+    turn_at = {}
+    multiply_at = {}
+    turn_r_at = {}
+    second_at = {}
+    order = [("o", 0), ("o", 1), ("w", 0, 0), ("w", 0, 1), ("w", 1, 0), ("w", 1, 1), ("o", 2), ("o", 3)]
+    order += [("w", a, h) for a in range(2, W_PAIRS) for h in range(2)]
+    for n, key in enumerate(order):
+        turn_at[n] = key
+    for g in range(GROUPS):
+        ready = order.index(("w", 2 * g + 1, 1))
+        for t in range(EARLY):
+            multiply_at[ready + 2 + t] = (t, g)
+    free = max(multiply_at) + 1
+    for i in range(EARLY, TILES):
+        first = free + GROUPS * (i - EARLY)
+        turn_at[first - 2] = ("o", i)
+        for g in range(GROUPS):
+            multiply_at[first + g] = (i, g)
+    step_of = {multiply_at[n]: n for n in multiply_at}
+    for i in range(TILES):
+        for h in range(2):
+            lag = R_LAG if i < TILES - 1 else 2
+            turn_r_at.setdefault(step_of[(i, 2 * h + 1)] + lag, []).append((i, h))
+    for i in range(TILES):
+        if i < EARLY:
+            n = free + S2_FIRST + 2 * i
+        elif i < TILES - 2:
+            n = step_of[(i + 2, S2_G)]
+        else:
+            n = step_of[(TILES - 1, 3)] + 1 + 2 * (i - TILES + 2)
+        second_at[n] = i
+    steps = max(second_at) + 3
+
+    load_order = [("o", 0), ("w", 0), ("w", 1), ("o", 1)]
+    load_order += [("w", a) for a in range(2, W_PAIRS)]
+    load_order += [("o", 2), ("D", 0), ("D", 1), ("o", 3)]
 
     with ExitStack() as ctx:
         const = ctx.enter_context(tc.tile_pool(name="const", bufs=1))
         raw_pool = ctx.enter_context(tc.tile_pool(name="raw", bufs=RAW_BUFS))
         stage = ctx.enter_context(tc.tile_pool(name="stage", bufs=2))
-        d_pool = ctx.enter_context(tc.tile_pool(name="dpool", bufs=4))
+        d_pool = ctx.enter_context(tc.tile_pool(name="dpool", bufs=6))
         psum = ctx.enter_context(tc.psum_pool(name="psum", bufs=2))
         ctx.enter_context(tc.manual_schedule())
 
@@ -66,9 +110,8 @@ def tile_originaltemporalsae_pa_kernel(tc, o, o_w, o_b, D, x, out_0, out_1):
         d_scales = const.tile([P, GROUPS, DIM], U8, align_bytes=64)
         x_sb = const.tile([P, TILES, DIM], BF16)
         ident = const.tile([P, P], F32)
-        bias_row = const.tile([P, WIDTH], BF16)
         ones = const.tile([P, P], BF16)
-        bias = const.tile([P, WIDTH], F32)
+        bias = const.tile([P, WIDTH], BF16)
         eps = const.tile([P, 1], F32)
         warm = const.tile([P, 1], F32)
         sum_sq = const.tile([P, TILES], F32)
@@ -94,77 +137,88 @@ def tile_originaltemporalsae_pa_kernel(tc, o, o_w, o_b, D, x, out_0, out_1):
             else:
                 nc.vector.tensor_copy(out=out, in_=in_)
 
-        def turn(key, t, h):
-            words = raw_tiles[key][:].bitcast(F32)
+        def row_words(key):
+            if key[0] == "o":
+                words = raw_tiles[("o", key[1] // 2)][:, key[1] % 2].bitcast(F32)
+                return words.rearrange("r (b w) -> r b w", b=2)
+            words = raw_tiles[("w", key[1])][:].bitcast(F32)
+            return words.rearrange("r b (h w) -> r h b w", h=2)[:, key[2]]
+
+        sorted_words = {}
+
+        def sort_words(key, engine):
+            words = stage.tile([P, 2, 2, 2 * P], F32, tag="words", bufs=4)
+            copy_out(engine, words[:], row_words(key).rearrange("r b (w u) -> r b u w", u=2))
+            sorted_words[key] = words
+
+        def turn(key, b):
             bank = psum.tile([P, 2, 2, P], F32, tag="tp", bufs=4)
             for s in range(2):
                 for u in range(2):
-                    c = 2 * h + s
-                    nc.tensor.transpose(
-                        bank[:, s, u], words[:, t, 2 * c * P + u : 2 * (c + 1) * P : 2], ident[:]
-                    )
+                    if key in sorted_words:
+                        in_ = sorted_words[key][:, b, u, s * P : (s + 1) * P]
+                    else:
+                        in_ = row_words(key)[:, b, 2 * s * P + u : 2 * (s + 1) * P : 2]
+                    nc.tensor.transpose(bank[:, s, u], in_, ident[:])
             return bank[:].rearrange("q s u m -> q s m u")
 
-        def prepare_o(i, h, engine):
-            turned = turn(("o", i // 2), i % 2, h)
-            grouped = stage.tile([P, 2, P, PACK], BF16, tag="grouped_o", align_bytes=64, bufs=3)
-            copy_out(engine, grouped[:].bitcast(F32), turned)
+        def prepare(key):
+            shape = [P, 2, 2, P, PACK]
+            grouped = stage.tile(shape, BF16, tag="grouped", align_bytes=64, bufs=3)
+            for b in range(2):
+                words = grouped[:].bitcast(F32)
+                words = words[:, b] if key[0] == "o" else words[:, :, b]
+                copy_out(COPY_T[b], words, turn(key, b))
 
             def quantise():
-                nc.vector.quantize_mx(
-                    out=o_codes[:, i, 2 * h : 2 * h + 2].rearrange("p c m -> p (c m)").bitcast(FP8X4),
-                    scales=o_scales[:, i, 2 * h : 2 * h + 2].rearrange("p c m -> p (c m)"),
-                    in_=grouped[:].rearrange("q c m t -> q (c m t)"),
-                )
+                if key[0] == "o":
+                    nc.vector.quantize_mx(
+                        out=o_codes[:, key[1]].rearrange("p c m -> p (c m)").bitcast(FP8X4),
+                        scales=o_scales[:, key[1]].rearrange("p c m -> p (c m)"),
+                        in_=grouped[:].rearrange("q b s m j -> q (b s m j)"),
+                    )
+                else:
+                    cols = slice(key[1] * PAIR, (key[1] + 1) * PAIR)
+                    for s in range(2):
+                        nc.vector.quantize_mx(
+                            out=w_codes[:, 2 * key[2] + s, cols].bitcast(FP8X4),
+                            scales=w_scales[:, 2 * key[2] + s, cols],
+                            in_=grouped[:, s].rearrange("q t m j -> q (t m j)"),
+                        )
 
             return quantise
 
-        def prepare_w(a, engines):
-            grouped = stage.tile([P, PASSES, PAIR, PACK], BF16, tag="grouped_w", align_bytes=64)
-            words = grouped[:].bitcast(F32)
-            for h in range(2):
-                for t in range(2):
-                    turned = turn(("w", a), t, h)
-                    copy_out(engines[2 * h + t], words[:, 2 * h : 2 * h + 2, t * P : (t + 1) * P], turned)
-            cols = slice(a * PAIR, (a + 1) * PAIR)
-            for c in range(PASSES):
-                nc.vector.quantize_mx(
-                    out=w_codes[:, c, cols].bitcast(FP8X4),
-                    scales=w_scales[:, c, cols],
-                    in_=grouped[:, c].rearrange("q m t -> q (m t)"),
-                )
-
-        grouped_d = {}
-
-        def regroup_d(g):
+        def prepare_d(g):
             raw = raw_tiles[("D", g // 2)]
-            grouped = stage.tile([P, DIM, PACK], BF16, tag="grouped_d", align_bytes=64)
+            grouped = stage.tile([P, DIM, PACK], BF16, tag="grouped_d", align_bytes=64, bufs=1)
             nc.vector.tensor_copy(
                 out=grouped[:].rearrange("p (c i) j -> p c j i", i=RUN),
                 in_=raw[:, g % 2].rearrange("p (j c i) -> p c j i", j=PACK, i=RUN),
             )
-            grouped_d[g] = grouped
 
-        def quantise_d(g):
-            nc.vector.quantize_mx(
-                out=d_codes[:, g].bitcast(FP8X4),
-                scales=d_scales[:, g],
-                in_=grouped_d[g][:].rearrange("p n j -> p (n j)"),
-            )
+            def quantise():
+                nc.vector.quantize_mx(
+                    out=d_codes[:, g].bitcast(FP8X4),
+                    scales=d_scales[:, g],
+                    in_=grouped[:].rearrange("p n j -> p (n j)"),
+                )
+
+            return quantise
 
         d_tiles = {}
         r_tiles = {}
         r_codes = {}
         r_scales = {}
+        accs = {}
+        dz_tiles = {}
 
-        def stage1(i, g):
+        def multiply(i, g):
             if g == 0:
                 d_tile = d_pool.tile([P, WIDTH], F32, tag="d")
                 d_tiles[i] = d_tile
-                r_tile = stage.tile([P, GROUPS, 2, P, 2], BF16, tag="r_bf", bufs=3)
-                r_tiles[i] = r_tile
             cols = slice(g * K_PASS, (g + 1) * K_PASS)
-            acc = psum.tile([P, K_PASS], F32, tag="acc")
+            acc = psum.tile([P, K_PASS], F32, tag="mm", bufs=4)
+            accs[(i, g)] = acc
             for c in range(PASSES):
                 nc.tensor.matmul_mx(
                     out=acc[:],
@@ -175,28 +229,36 @@ def tile_originaltemporalsae_pa_kernel(tc, o, o_w, o_b, D, x, out_0, out_1):
                     start=(c == 0),
                     stop=(c == PASSES - 1),
                 )
-            nc.vector.tensor_tensor(out=d_tiles[i][:, cols], in0=acc[:], in1=bias[:, cols], op=ALU.add)
+
+        def add_bias(i, g):
+            cols = slice(g * K_PASS, (g + 1) * K_PASS)
+            nc.vector.tensor_tensor(
+                out=d_tiles[i][:, cols], in0=accs[(i, g)][:], in1=bias[:, cols], op=ALU.add
+            )
 
         def relu(i, g):
             cols = slice(g * K_PASS, (g + 1) * K_PASS)
+            if g % 2 == 0:
+                r_tile = stage.tile([P, 2, 2, P, 2], BF16, tag="r_bf", bufs=7)
+                r_tiles[(i, g // 2)] = r_tile
             nc.scalar.activation(
-                out=r_tiles[i][:, g],
+                out=r_tiles[(i, g // 2)][:, g % 2],
                 in_=d_tiles[i][:, cols].rearrange("r (w u e) -> r u w e", u=2, e=2),
                 func=ACT.Relu,
             )
 
-        def turn_r(i, h, engine):
-            words = r_tiles[i][:].rearrange("r g u w e -> r (g u w e)").bitcast(F32)
+        def turn_r(i, h):
+            words = r_tiles[(i, h)][:].rearrange("r s u w e -> r (s u w e)").bitcast(F32)
             bank = psum.tile([P, 2, 2, P], F32, tag="tp", bufs=4)
             for s in range(2):
                 for u in range(2):
-                    first = ((2 * h + s) * 2 + u) * P
+                    first = (s * 2 + u) * P
                     nc.tensor.transpose(bank[:, s, u], words[:, first : first + P], ident[:])
             grouped = stage.tile([P, 2, P, PACK], BF16, tag="grouped_r", align_bytes=64)
-            copy_out(engine, grouped[:].bitcast(F32), bank[:].rearrange("q s u m -> q s m u"))
+            copy_out("S", grouped[:].bitcast(F32), bank[:].rearrange("q s u m -> q s m u"))
             if h == 0:
-                codes = stage.tile([P, GROUPS, P], U32, tag="r_codes", align_bytes=64)
-                scales = stage.tile([P, GROUPS, P], U8, tag="r_scales", align_bytes=64)
+                codes = stage.tile([P, GROUPS, P], U32, tag="r_codes", align_bytes=64, bufs=5)
+                scales = stage.tile([P, GROUPS, P], U8, tag="r_scales", align_bytes=64, bufs=5)
                 r_codes[i] = codes
                 r_scales[i] = scales
 
@@ -209,10 +271,8 @@ def tile_originaltemporalsae_pa_kernel(tc, o, o_w, o_b, D, x, out_0, out_1):
 
             return quantise
 
-        dz_tiles = {}
-
-        def stage2(i):
-            dz = psum.tile([P, DIM], F32, tag="dz")
+        def second(i):
+            dz = psum.tile([P, DIM], F32, tag="mm", bufs=4)
             dz_tiles[i] = dz
             for g in range(GROUPS):
                 nc.tensor.matmul_mx(
@@ -225,16 +285,16 @@ def tile_originaltemporalsae_pa_kernel(tc, o, o_w, o_b, D, x, out_0, out_1):
                     stop=(g == GROUPS - 1),
                 )
 
-        def squares(i):
-            squared = stage.tile([P, DIM], F32, tag="squares")
+        def square(i):
+            squared = stage.tile([P, DIM], F32, tag="squared", bufs=1)
             nc.scalar.activation(
                 out=squared[:], in_=dz_tiles[i][:], func=ACT.Square, accum_out=sum_sq[:, i : i + 1]
             )
 
-        def products(i):
-            product = stage.tile([P, DIM], F32, tag="products")
+        def product(i):
+            multiplied = stage.tile([P, DIM], F32, tag="multiplied", bufs=1)
             nc.vector.scalar_tensor_tensor(
-                out=product[:],
+                out=multiplied[:],
                 in0=dz_tiles[i][:],
                 scalar=1.0,
                 in1=x_sb[:, i],
@@ -253,24 +313,27 @@ def tile_originaltemporalsae_pa_kernel(tc, o, o_w, o_b, D, x, out_0, out_1):
             nc.vector.reciprocal(out=inv[:, one], in_=norm_sq[:, one])
             nc.vector.tensor_tensor(out=proj[:, one], in0=dot[:, one], in1=inv[:, one], op=ALU.mult)
 
-        def finish(i):
+        def make_x_pred(i):
             one = slice(i, i + 1)
             rows = slice(i * P, (i + 1) * P)
             x_pred = stage.tile([P, DIM], F32, tag="x_pred")
             nc.scalar.activation(out=x_pred[:], in_=dz_tiles[i][:], func=ACT.Copy, scale=proj[:, one])
             nc.sync.dma_start(out=xp_rows[rows, :], in_=x_pred[:])
-            for h in range(2):
-                cols = slice(h * WIDTH // 2, (h + 1) * WIDTH // 2)
-                nc.vector.tensor_scalar(
-                    out=d_tiles[i][:, cols],
-                    in0=d_tiles[i][:, cols],
-                    scalar1=0.0,
-                    scalar2=proj[:, one],
-                    op0=ALU.max,
-                    op1=ALU.mult,
-                )
-                nc.sync.dma_start(out=z_rows[rows, cols], in_=d_tiles[i][:, cols])
 
+        def make_z(i, h):
+            rows = slice(i * P, (i + 1) * P)
+            cols = slice(h * WIDTH // 2, (h + 1) * WIDTH // 2)
+            nc.vector.tensor_scalar(
+                out=d_tiles[i][:, cols],
+                in0=d_tiles[i][:, cols],
+                scalar1=0.0,
+                scalar2=proj[:, i : i + 1],
+                op0=ALU.max,
+                op1=ALU.mult,
+            )
+            nc.sync.dma_start(out=z_rows[rows, cols], in_=d_tiles[i][:, cols])
+
+        bias_row = stage.tile([P, WIDTH], BF16, tag="words", bufs=4)
         nc.vector.memset(bias_row[:], 0.0)
         nc.vector.memset(ones[:], 1.0)
         nc.vector.memset(eps[:], EPS)
@@ -281,79 +344,66 @@ def tile_originaltemporalsae_pa_kernel(tc, o, o_w, o_b, D, x, out_0, out_1):
             load_next()
         make_identity(nc, ident[:])
 
-        for t in range(EARLY):
-            for h in range(2):
-                prepare_o(t, h, "SV"[h])()
-        load_next()
-        for a in range(W_PAIRS + EARLY):
-            if a < W_PAIRS:
-                prepare_w(a, "SSSV" if a < 5 else "SSSS")
-            else:
-                for h in range(2):
-                    prepare_o(a - W_PAIRS + EARLY, h, "SV"[h])()
-            load_next()
-            if a == 0:
-                for g in range(GROUPS):
-                    cols = slice(g * K_PASS, (g + 1) * K_PASS)
-                    bank = psum.tile([P, K_PASS], F32, tag=("acc", "dz")[g // 2])
-                    nc.tensor.matmul(bank[:], lhsT=ones[:], rhs=bias_row[:, cols], start=True, stop=True)
-                    copy_out("SV"[g % 2], bias[:, cols], bank[:])
-            if a >= 3:
-                relu((a - 1) % 2, (a - 3) // 2)
-            if a in (7, 8):
-                turn_r(a - 7, 0, "S")()
-            if a >= 2:
-                stage1(a % 2, (a - 2) // 2)
-            if 0 <= a - 6 < GROUPS:
-                quantise_d(a - 6)
-            if 0 <= a - 5 < GROUPS:
-                regroup_d(a - 5)
-        nc.sync.dma_start(out=x_sb[:], in_=x_rows.rearrange("(t p) n -> p t n", p=P))
-        relu(1, GROUPS - 1)
+        def spread_bias(g):
+            cols = slice(g * K_PASS, (g + 1) * K_PASS)
+            bank = psum.tile([P, K_PASS], F32, tag="mm", bufs=4)
+            nc.tensor.matmul(bank[:], lhsT=ones[:], rhs=bias_row[:, cols], start=True, stop=True)
+            copy_out("SV"[g % 2], bias[:, cols], bank[:])
 
-        for i in range(EARLY, TILES):
-            for h in range(2):
-                if i == EARLY:
-                    turned_r = (h, 1)
-                    done = (None, 0)[h]
-                    old = None
-                else:
-                    turned_r = (i - 1, h)
-                    done = (i - 2, None)[h]
-                    old = (i - 3 if i == EARLY + 1 else None, i - 2)[h]
-                ready = []
-                if i + 2 < TILES:
-                    ready.append(prepare_o(i + 2, h, "S"))
-                ready.append(turn_r(turned_r[0], turned_r[1], "S"))
-                if old is not None:
-                    finish(old)
-                if done is not None:
-                    stage2(done)
-                    squares(done)
-                stage1(i, 2 * h)
-                relu(i, 2 * h)
-                if done is not None:
-                    products(done)
-                    norms(done)
-                for quantise in ready:
-                    quantise()
-                stage1(i, 2 * h + 1)
-                relu(i, 2 * h + 1)
-                if done is not None:
-                    project(done)
+        def sort_engine(key):
+            return SORT_O if key[0] == "o" else SORT_W[key[2]]
 
-        last = TILES - 1
-        turn_r(last, 0, "S")()
-        stage2(last - 1)
-        squares(last - 1)
-        turn_r(last, 1, "V")()
-        products(last - 1)
-        norms(last - 1)
-        stage2(last)
-        project(last - 1)
-        squares(last)
-        finish(last - 1)
-        products(last)
-        norms(last)
-        project(last)
-        finish(last)
+        def is_sorted(n):
+            return n in turn_at and (turn_at[n][0] == "o" and turn_at[n][1] >= 4 or n >= FIRST_SORT and turn_at[n][0] == "w" and n % 4 in SORT_SET)
+
+        used = {}
+        for n in turn_at:
+            key = turn_at[n]
+            raw = ("o", key[1] // 2) if key[0] == "o" else key[:2]
+            last_use = n - LEAD if is_sorted(n) else n
+            used[raw] = max(used.get(raw, 0), last_use)
+        for g in range(GROUPS):
+            used[("D", g // 2)] = D_FIRST + D_STEP * (g // 2 * 2 + 1)
+
+        d_ready = []
+        for n in range(steps):
+            before = multiply_at.get(n - 1)
+            second_before = second_at.get(n - 1)
+            quantises = []
+            if second_before is not None:
+                norms(second_before)
+            if is_sorted(n + LEAD):
+                sort_words(turn_at[n + LEAD], sort_engine(turn_at[n + LEAD]))
+            if n in turn_at:
+                quantises.append(prepare(turn_at[n]))
+            for i, h in turn_r_at.get(n, []):
+                quantises.append(turn_r(i, h))
+            if 2 <= n < 2 + GROUPS:
+                spread_bias(n - 2)
+            if n in second_at:
+                second(second_at[n])
+            if n in multiply_at:
+                multiply(multiply_at[n][0], multiply_at[n][1])
+            if before is not None:
+                add_bias(before[0], before[1])
+                relu(before[0], before[1])
+            if second_before is not None:
+                product(second_before)
+                project(second_before)
+                make_x_pred(second_before)
+            if n in second_at:
+                square(second_at[n])
+            for quantise in d_ready + quantises:
+                quantise()
+            d_ready = []
+            if second_before is not None:
+                make_z(second_before, 0)
+            if n - 2 in second_at:
+                make_z(second_at[n - 2], 1)
+            if n >= D_FIRST and (n - D_FIRST) % D_STEP == 0 and (n - D_FIRST) // D_STEP < GROUPS:
+                d_ready.append(prepare_d((n - D_FIRST) // D_STEP))
+            for raw in load_order:
+                if used[raw] == n:
+                    load_next()
+            if n == D_FIRST + 2:
+                nc.sync.dma_start(out=x_sb[:], in_=x_rows.rearrange("(t p) n -> p t n", p=P))

@@ -68,7 +68,7 @@ def tile_originaltemporalsae_pa_kernel(tc, o, o_w, o_b, D, x, out_0, out_1):
     for g in range(GROUPS):
         ready = order.index(("w", 2 * g + 1, 1))
         for t in range(EARLY):
-            multiply_at[ready + 2 + t] = (t, g)
+            multiply_at[ready + 2 + t + (max(t - 1, 0) if g == 0 else 0)] = (t, g)
     free = max(multiply_at) + 1
     for i in range(EARLY, TILES):
         first = free + GROUPS * (i - EARLY)
@@ -78,17 +78,18 @@ def tile_originaltemporalsae_pa_kernel(tc, o, o_w, o_b, D, x, out_0, out_1):
     step_of = {multiply_at[n]: n for n in multiply_at}
     for i in range(TILES):
         for h in range(2):
-            lag = R_LAG if i < TILES - 1 else 2
-            turn_r_at.setdefault(step_of[(i, 2 * h + 1)] + lag, []).append((i, h))
-    for i in range(TILES):
+            if i < TILES - 1:
+                lag = 2 if (i, h) == (TILES - 2, 1) else R_LAG
+                turn_r_at.setdefault(step_of[(i, 2 * h + 1)] + lag, []).append((i, h))
+    for i in range(TILES - 1):
         if i < EARLY:
             n = free + S2_FIRST + 2 * i
         elif i < TILES - 2:
             n = step_of[(i + 2, S2_G)]
         else:
-            n = step_of[(TILES - 1, 3)] + 1 + 2 * (i - TILES + 2)
+            n = step_of[(i + 1, 2)]
         second_at[n] = i
-    steps = max(second_at) + 3
+    steps = step_of[(TILES - 1, GROUPS - 1)]
 
     load_order = [("o", 0), ("w", 0), ("w", 1), ("o", 1)]
     load_order += [("w", a) for a in range(2, W_PAIRS)]
@@ -111,6 +112,7 @@ def tile_originaltemporalsae_pa_kernel(tc, o, o_w, o_b, D, x, out_0, out_1):
         x_sb = const.tile([P, TILES, DIM], BF16)
         ident = const.tile([P, P], F32)
         ones = const.tile([P, P], BF16)
+        zeros = const.tile([P, K_PASS], BF16)
         bias = const.tile([P, WIDTH], BF16)
         eps = const.tile([P, 1], F32)
         warm = const.tile([P, 1], F32)
@@ -212,13 +214,13 @@ def tile_originaltemporalsae_pa_kernel(tc, o, o_w, o_b, D, x, out_0, out_1):
         accs = {}
         dz_tiles = {}
 
-        def multiply(i, g):
+        def multiply(i, g, first=0, width=K_PASS):
             if g == 0:
                 d_tile = d_pool.tile([P, WIDTH], F32, tag="d")
                 d_tiles[i] = d_tile
-            cols = slice(g * K_PASS, (g + 1) * K_PASS)
-            acc = psum.tile([P, K_PASS], F32, tag="mm", bufs=4)
-            accs[(i, g)] = acc
+            cols = slice(g * K_PASS + first, g * K_PASS + first + width)
+            acc = psum.tile([P, width], F32, tag="mm", bufs=4)
+            accs[(i, g, first)] = acc
             for c in range(PASSES):
                 nc.tensor.matmul_mx(
                     out=acc[:],
@@ -230,32 +232,34 @@ def tile_originaltemporalsae_pa_kernel(tc, o, o_w, o_b, D, x, out_0, out_1):
                     stop=(c == PASSES - 1),
                 )
 
-        def add_bias(i, g):
-            cols = slice(g * K_PASS, (g + 1) * K_PASS)
+        def add_bias(i, g, first=0, width=K_PASS):
+            cols = slice(g * K_PASS + first, g * K_PASS + first + width)
             nc.vector.tensor_tensor(
-                out=d_tiles[i][:, cols], in0=accs[(i, g)][:], in1=bias[:, cols], op=ALU.add
+                out=d_tiles[i][:, cols], in0=accs[(i, g, first)][:], in1=bias[:, cols], op=ALU.add
             )
 
-        def relu(i, g):
-            cols = slice(g * K_PASS, (g + 1) * K_PASS)
+        def relu(i, g, first=0, width=K_PASS):
+            cols = slice(g * K_PASS + first, g * K_PASS + first + width)
+            pairs = slice(first // PACK, (first + width) // PACK)
             if g % 2 == 0:
                 r_tile = stage.tile([P, 2, 2, P, 2], BF16, tag="r_bf", bufs=7)
                 r_tiles[(i, g // 2)] = r_tile
             nc.scalar.activation(
-                out=r_tiles[(i, g // 2)][:, g % 2],
+                out=r_tiles[(i, g // 2)][:, g % 2, :, pairs],
                 in_=d_tiles[i][:, cols].rearrange("r (w u e) -> r u w e", u=2, e=2),
                 func=ACT.Relu,
             )
 
-        def turn_r(i, h):
+        def turn_r(i, h, places=(0, 1)):
             words = r_tiles[(i, h)][:].rearrange("r s u w e -> r (s u w e)").bitcast(F32)
-            bank = psum.tile([P, 2, 2, P], F32, tag="tp", bufs=4)
-            for s in range(2):
+            bank = psum.tile([P, len(places), 2, P], F32, tag="tp", bufs=4)
+            for k, s in enumerate(places):
                 for u in range(2):
                     first = (s * 2 + u) * P
-                    nc.tensor.transpose(bank[:, s, u], words[:, first : first + P], ident[:])
-            grouped = stage.tile([P, 2, P, PACK], BF16, tag="grouped_r", align_bytes=64)
+                    nc.tensor.transpose(bank[:, k, u], words[:, first : first + P], ident[:])
+            grouped = stage.tile([P, len(places), P, PACK], BF16, tag="grouped_r", align_bytes=64)
             copy_out("S", grouped[:].bitcast(F32), bank[:].rearrange("q s u m -> q s m u"))
+            groups = slice(2 * h + places[0], 2 * h + places[-1] + 1)
             if h == 0:
                 codes = stage.tile([P, GROUPS, P], U32, tag="r_codes", align_bytes=64, bufs=5)
                 scales = stage.tile([P, GROUPS, P], U8, tag="r_scales", align_bytes=64, bufs=5)
@@ -264,8 +268,8 @@ def tile_originaltemporalsae_pa_kernel(tc, o, o_w, o_b, D, x, out_0, out_1):
 
             def quantise():
                 nc.vector.quantize_mx(
-                    out=r_codes[i][:, 2 * h : 2 * h + 2].rearrange("p g m -> p (g m)").bitcast(FP8X4),
-                    scales=r_scales[i][:, 2 * h : 2 * h + 2].rearrange("p g m -> p (g m)"),
+                    out=r_codes[i][:, groups].rearrange("p g m -> p (g m)").bitcast(FP8X4),
+                    scales=r_scales[i][:, groups].rearrange("p g m -> p (g m)"),
                     in_=grouped[:].rearrange("q g m t -> q (g m t)"),
                 )
 
@@ -334,8 +338,9 @@ def tile_originaltemporalsae_pa_kernel(tc, o, o_w, o_b, D, x, out_0, out_1):
             nc.sync.dma_start(out=z_rows[rows, cols], in_=d_tiles[i][:, cols])
 
         bias_row = stage.tile([P, WIDTH], BF16, tag="words", bufs=4)
-        nc.vector.memset(bias_row[:], 0.0)
         nc.vector.memset(ones[:], 1.0)
+        nc.vector.memset(zeros[:], 0.0)
+        nc.vector.memset(bias_row[:], 0.0)
         nc.vector.memset(eps[:], EPS)
         nc.scalar.activation(out=warm[:], in_=eps[:], func=ACT.Sqrt)
         load_next()
@@ -343,6 +348,11 @@ def tile_originaltemporalsae_pa_kernel(tc, o, o_w, o_b, D, x, out_0, out_1):
         for k in range(RAW_BUFS - 1):
             load_next()
         make_identity(nc, ident[:])
+
+        def keep_warm(count):
+            idle = psum.tile([P, K_PASS], F32, tag="mm", bufs=4)
+            for k in range(count):
+                nc.tensor.matmul(idle[:], lhsT=ones[:], rhs=zeros[:], start=True, stop=True)
 
         def spread_bias(g):
             cols = slice(g * K_PASS, (g + 1) * K_PASS)
@@ -365,6 +375,8 @@ def tile_originaltemporalsae_pa_kernel(tc, o, o_w, o_b, D, x, out_0, out_1):
         for g in range(GROUPS):
             used[("D", g // 2)] = D_FIRST + D_STEP * (g // 2 * 2 + 1)
 
+        ready_first = min(multiply_at)
+        keep_warm(4)
         d_ready = []
         for n in range(steps):
             before = multiply_at.get(n - 1)
@@ -380,6 +392,8 @@ def tile_originaltemporalsae_pa_kernel(tc, o, o_w, o_b, D, x, out_0, out_1):
                 quantises.append(turn_r(i, h))
             if 2 <= n < 2 + GROUPS:
                 spread_bias(n - 2)
+            if n < ready_first - 1:
+                keep_warm(1)
             if n in second_at:
                 second(second_at[n])
             if n in multiply_at:
@@ -407,3 +421,91 @@ def tile_originaltemporalsae_pa_kernel(tc, o, o_w, o_b, D, x, out_0, out_1):
                     load_next()
             if n == D_FIRST + 2:
                 nc.sync.dma_start(out=x_sb[:], in_=x_rows.rearrange("(t p) n -> p t n", p=P))
+
+        i = TILES - 1
+        half = K_PASS // 2
+        quantise_a = turn_r(i, 0)
+        multiply(i, 3, 0, half)
+        multiply(i, 3, half, half)
+        add_bias(i, 2)
+        relu(i, 2)
+        add_bias(i, 3, 0, half)
+        relu(i, 3, 0, half)
+        add_bias(i, 3, half, half)
+        relu(i, 3, half, half)
+        norms(i - 1)
+        quantise_a()
+        product(i - 1)
+        project(i - 1)
+        quantise_b = turn_r(i, 1, (0,))
+        quantise_c = turn_r(i, 1, (1,))
+        quantise_b()
+        dz_halves = []
+        for k in range(2):
+            dz_half = psum.tile([P, half], F32, tag="tp", bufs=4)
+            dz_halves.append(dz_half)
+        for g in range(GROUPS):
+            if g == GROUPS - 1:
+                quantise_c()
+            for k in range(2):
+                cols = slice(k * half, (k + 1) * half)
+                nc.tensor.matmul_mx(
+                    out=dz_halves[k][:],
+                    lhsT=r_codes[i][:, g].bitcast(FP8X4),
+                    lhsT_scale=r_scales[i][:, g],
+                    rhs=d_codes[:, g, cols].bitcast(FP8X4),
+                    rhs_scale=d_scales[:, g, cols],
+                    start=(g == 0),
+                    stop=(g == GROUPS - 1),
+                )
+        make_x_pred(i - 1)
+        make_z(i - 1, 0)
+        make_z(i - 1, 1)
+        sum_sq_half = const.tile([P, 2], F32)
+        dot_half = const.tile([P, 2], F32)
+        squared = stage.tile([P, DIM], F32, tag="squared", bufs=1)
+        multiplied = stage.tile([P, DIM], F32, tag="multiplied", bufs=1)
+        for k in range(2):
+            nc.scalar.activation(
+                out=squared[:, k * half : (k + 1) * half],
+                in_=dz_halves[k][:],
+                func=ACT.Square,
+                accum_out=sum_sq_half[:, k : k + 1],
+            )
+            nc.vector.scalar_tensor_tensor(
+                out=multiplied[:, k * half : (k + 1) * half],
+                in0=dz_halves[1 - k][:],
+                scalar=1.0,
+                in1=x_sb[:, i, (1 - k) * half : (2 - k) * half],
+                op0=ALU.mult,
+                op1=ALU.mult,
+                accum_out=dot_half[:, k : k + 1],
+            )
+        one = slice(i, i + 1)
+        rows = slice(i * P, (i + 1) * P)
+        nc.scalar.activation(
+            out=norm[:, one], in_=sum_sq_half[:, 0:1], func=ACT.Sqrt, bias=sum_sq_half[:, 1:2]
+        )
+        nc.vector.tensor_tensor(out=dot[:, one], in0=dot_half[:, 0:1], in1=dot_half[:, 1:2], op=ALU.add)
+        nc.scalar.activation(out=norm_sq[:, one], in_=norm[:, one], func=ACT.Square, bias=eps[:, 0:1])
+        project(i)
+        x_pred = stage.tile([P, DIM], F32, tag="x_pred")
+        for k in range(2):
+            nc.scalar.activation(
+                out=x_pred[:, k * half : (k + 1) * half],
+                in_=dz_halves[k][:],
+                func=ACT.Copy,
+                scale=proj[:, one],
+            )
+        for k in range(GROUPS):
+            cols = slice(k * K_PASS, (k + 1) * K_PASS)
+            nc.vector.tensor_scalar(
+                out=d_tiles[i][:, cols],
+                in0=d_tiles[i][:, cols],
+                scalar1=0.0,
+                scalar2=proj[:, one],
+                op0=ALU.max,
+                op1=ALU.mult,
+            )
+            nc.sync.dma_start(out=z_rows[rows, cols], in_=d_tiles[i][:, cols])
+        nc.sync.dma_start(out=xp_rows[rows, :], in_=x_pred[:])

@@ -20,24 +20,23 @@ WIDTH = 2048
 DIM = 512
 PASSES = WIDTH // K_PASS
 GROUPS = WIDTH // K_PASS
-PAIR = 2 * P
-W_PAIRS = WIDTH // PAIR
+BLOCKS = WIDTH // P
 EPS = 1e-6
 RAW_BUFS = 4
 RUN = 4
-EARLY = 4
-SORT_W = ("V", "V")
-SORT_O = "V"
-COPY_T = ("S", "S")
-FIRST_SORT = 6
+CHUNKS = ((0, 4), (4, 2), (6, 1), (7, 1))
 LEAD = 2
-R_LAG = 3
-S2_FIRST = 1
-S2_G = 0
-D_FIRST = 18
-D_STEP = 2
-SORT_SET = (0, 1, 2, 3)
-D_LOAD = 10
+O_SORT = 5
+LAG = 2
+O_FIRST = 3
+FIRST_SORT = 5
+NO_SORT = ()
+D_AT = (18, 20, 21, 22)
+D_ENGINES = "VSVS"
+S2_FIRST = 27
+S2_NUM = 5
+Z_LAG = 2
+WARM = (0, 1, 2, 3, 4, 5)
 
 FLOPS = 2 * ROWS * WIDTH * WIDTH + 2 * ROWS * WIDTH * DIM
 
@@ -50,71 +49,66 @@ def tile_originaltemporalsae_pa_kernel(tc, o, o_w, o_b, D, x, out_0, out_1):
     xp_rows = out_1.flatten_outer_dims()
 
     views = {}
-    for a in range(ROWS // PAIR):
+    for a in range(TILES // 2):
         views[("o", a)] = o_rows.rearrange("(a t p) k -> a p t k", t=2, p=P)[a]
-    for a in range(W_PAIRS):
-        views[("w", a)] = o_w.rearrange("(a t p) k -> a p t k", t=2, p=P)[a]
+    for a in range(BLOCKS // 2):
+        views[("w", a)] = o_w.rearrange("(a p h t) k -> a h p t k", p=P, h=2, t=2)[a // 2, a % 2]
     for a in range(GROUPS // 2):
         views[("D", a)] = D.rearrange("(a g p j) n -> a p g (j n)", g=2, p=P, j=PACK)[a]
 
     turn_at = {}
-    multiply_at = {}
-    turn_r_at = {}
+    unit_at = {}
+    unit_step = {}
     second_at = {}
-    order = [("o", 0), ("o", 1), ("w", 0, 0), ("w", 0, 1), ("w", 1, 0), ("w", 1, 1), ("o", 2), ("o", 3)]
-    order += [("w", a, h) for a in range(2, W_PAIRS) for h in range(2)]
+    z_at = {}
+    early = CHUNKS[0][1]
+    order = [("o", i) for i in range(early)] + [("w", m) for m in range(BLOCKS)]
     for n, key in enumerate(order):
-        turn_at[n] = key
-    for g in range(GROUPS):
-        ready = order.index(("w", 2 * g + 1, 1))
-        for t in range(EARLY):
-            multiply_at[ready + 2 + t + (max(t - 1, 0) if g == 0 else 0)] = (t, g)
-    free = max(multiply_at) + 1
-    for i in range(EARLY, TILES):
-        first = free + GROUPS * (i - EARLY)
-        turn_at[first - 2] = ("o", i)
-        for g in range(GROUPS):
-            multiply_at[first + g] = (i, g)
-    step_of = {multiply_at[n]: n for n in multiply_at}
-    for i in range(TILES):
-        for h in range(2):
-            if i < TILES - 1:
-                lag = 2 if (i, h) == (TILES - 2, 1) else R_LAG
-                turn_r_at.setdefault(step_of[(i, 2 * h + 1)] + lag, []).append((i, h))
+        turn_at.setdefault(n, []).append(key)
+    n = early + LAG
+    for q, (first, tiles) in enumerate(CHUNKS):
+        blocks = early // tiles
+        if q > 0:
+            for t in range(tiles):
+                turn_at.setdefault(n - O_FIRST + t, []).append(("o", first + t))
+        for m in range(0, BLOCKS, blocks):
+            unit_at[n] = (q, m, blocks)
+            unit_step[(q, m + blocks - 1)] = n
+            n += 1
     for i in range(TILES - 1):
-        if i < EARLY:
-            n = free + S2_FIRST + 2 * i
-        elif i < TILES - 2:
-            n = step_of[(i + 2, S2_G)]
-        else:
-            n = step_of[(i + 1, 2)]
-        second_at[n] = i
-    steps = step_of[(TILES - 1, GROUPS - 1)]
+        second_at[S2_FIRST + S2_NUM * i // 3] = i
+    for n in second_at:
+        for g in range(GROUPS):
+            z_at.setdefault(n + Z_LAG + g // 2, []).append((second_at[n], g))
+    regroup_at = {}
+    for q in range(len(CHUNKS)):
+        for g in range(GROUPS):
+            regroup_at.setdefault(unit_step[(q, PACK * g + PACK - 1)] + 2, []).append((q, g))
+    steps = max(unit_at)
 
-    load_order = [("o", 0), ("w", 0), ("w", 1), ("o", 1)]
-    load_order += [("w", a) for a in range(2, W_PAIRS)]
-    load_order += [("o", 2), ("D", 0), ("D", 1), ("o", 3)]
+    load_order = [("o", 0), ("o", 1)] + [("w", a) for a in range(BLOCKS // 2)]
+    load_order += [("o", 2), ("o", 3), ("D", 0), ("D", 1)]
 
     with ExitStack() as ctx:
         const = ctx.enter_context(tc.tile_pool(name="const", bufs=1))
         raw_pool = ctx.enter_context(tc.tile_pool(name="raw", bufs=RAW_BUFS))
         stage = ctx.enter_context(tc.tile_pool(name="stage", bufs=2))
-        d_pool = ctx.enter_context(tc.tile_pool(name="dpool", bufs=6))
-        psum = ctx.enter_context(tc.psum_pool(name="psum", bufs=2))
+        relu_pool = ctx.enter_context(tc.tile_pool(name="relu", bufs=GROUPS))
+        psum = ctx.enter_context(tc.psum_pool(name="psum", bufs=4))
         ctx.enter_context(tc.manual_schedule())
 
-        w_codes = const.tile([P, PASSES, WIDTH], U32, align_bytes=64)
-        w_scales = const.tile([P, PASSES, WIDTH], U8, align_bytes=64)
-        o_codes = const.tile([P, TILES, PASSES, P], U32, align_bytes=64)
-        o_scales = const.tile([P, TILES, PASSES, P], U8, align_bytes=64)
+        w_codes = const.tile([P, BLOCKS, PASSES, P], U32, align_bytes=64)
+        w_scales = const.tile([P, BLOCKS, PASSES, P], U8, align_bytes=64)
+        o_codes = const.tile([P, PASSES, ROWS], U32, align_bytes=64)
+        o_scales = const.tile([P, PASSES, ROWS], U8, align_bytes=64)
         d_codes = const.tile([P, GROUPS, DIM], U32, align_bytes=64)
         d_scales = const.tile([P, GROUPS, DIM], U8, align_bytes=64)
         x_sb = const.tile([P, TILES, DIM], BF16)
         ident = const.tile([P, P], F32)
-        ones = const.tile([P, P], BF16)
-        zeros = const.tile([P, K_PASS], BF16)
-        bias = const.tile([P, WIDTH], BF16)
+        bias_raw = const.tile([P, GROUPS, PACK], BF16)
+        bias = const.tile([P, BLOCKS], F32)
         eps = const.tile([P, 1], F32)
+        zeros = const.tile([P, K_PASS], BF16)
         warm = const.tile([P, 1], F32)
         sum_sq = const.tile([P, TILES], F32)
         norm = const.tile([P, TILES], F32)
@@ -140,62 +134,55 @@ def tile_originaltemporalsae_pa_kernel(tc, o, o_w, o_b, D, x, out_0, out_1):
                 nc.vector.tensor_copy(out=out, in_=in_)
 
         def row_words(key):
-            if key[0] == "o":
-                words = raw_tiles[("o", key[1] // 2)][:, key[1] % 2].bitcast(F32)
-                return words.rearrange("r (b w) -> r b w", b=2)
-            words = raw_tiles[("w", key[1])][:].bitcast(F32)
-            return words.rearrange("r b (h w) -> r h b w", h=2)[:, key[2]]
+            return raw_tiles[(key[0], key[1] // 2)][:, key[1] % 2].bitcast(F32)
 
         sorted_words = {}
 
-        def sort_words(key, engine):
-            words = stage.tile([P, 2, 2, 2 * P], F32, tag="words", bufs=4)
-            copy_out(engine, words[:], row_words(key).rearrange("r b (w u) -> r b u w", u=2))
+        def sort_words(key):
+            words = stage.tile([P, 2, WIDTH // 4], F32, tag="words", bufs=4)
+            nc.vector.tensor_copy(out=words[:], in_=row_words(key).rearrange("r (w u) -> r u w", u=2))
             sorted_words[key] = words
 
-        def turn(key, b):
-            bank = psum.tile([P, 2, 2, P], F32, tag="tp", bufs=4)
-            for s in range(2):
-                for u in range(2):
-                    if key in sorted_words:
-                        in_ = sorted_words[key][:, b, u, s * P : (s + 1) * P]
-                    else:
-                        in_ = row_words(key)[:, b, 2 * s * P + u : 2 * (s + 1) * P : 2]
-                    nc.tensor.transpose(bank[:, s, u], in_, ident[:])
-            return bank[:].rearrange("q s u m -> q s m u")
-
         def prepare(key):
-            shape = [P, 2, 2, P, PACK]
-            grouped = stage.tile(shape, BF16, tag="grouped", align_bytes=64, bufs=3)
-            for b in range(2):
-                words = grouped[:].bitcast(F32)
-                words = words[:, b] if key[0] == "o" else words[:, :, b]
-                copy_out(COPY_T[b], words, turn(key, b))
+            grouped = stage.tile([P, PASSES, P, PACK], BF16, tag="grouped", align_bytes=64, bufs=3)
+            words = grouped[:].bitcast(F32)
+            for b in range(PASSES // 2):
+                bank = psum.tile([P, 2, 2, P], F32, tag="tp")
+                for s in range(2):
+                    c = 2 * b + s
+                    for u in range(2):
+                        if key in sorted_words:
+                            in_ = sorted_words[key][:, u, c * P : (c + 1) * P]
+                        else:
+                            in_ = row_words(key)[:, 2 * c * P + u : 2 * (c + 1) * P : 2]
+                        nc.tensor.transpose(bank[:, s, u], in_, ident[:])
+                copy_out("S", words[:, 2 * b : 2 * b + 2], bank[:].rearrange("q s u m -> q s m u"))
 
             def quantise():
-                if key[0] == "o":
+                if key[0] == "w":
                     nc.vector.quantize_mx(
-                        out=o_codes[:, key[1]].rearrange("p c m -> p (c m)").bitcast(FP8X4),
-                        scales=o_scales[:, key[1]].rearrange("p c m -> p (c m)"),
-                        in_=grouped[:].rearrange("q b s m j -> q (b s m j)"),
+                        out=w_codes[:, key[1]].rearrange("q c m -> q (c m)").bitcast(FP8X4),
+                        scales=w_scales[:, key[1]].rearrange("q c m -> q (c m)"),
+                        in_=grouped[:].rearrange("q c m j -> q (c m j)"),
                     )
                 else:
-                    cols = slice(key[1] * PAIR, (key[1] + 1) * PAIR)
-                    for s in range(2):
+                    cols = slice(key[1] * P, (key[1] + 1) * P)
+                    for c in range(PASSES):
                         nc.vector.quantize_mx(
-                            out=w_codes[:, 2 * key[2] + s, cols].bitcast(FP8X4),
-                            scales=w_scales[:, 2 * key[2] + s, cols],
-                            in_=grouped[:, s].rearrange("q t m j -> q (t m j)"),
+                            out=o_codes[:, c, cols].bitcast(FP8X4),
+                            scales=o_scales[:, c, cols],
+                            in_=grouped[:, c].rearrange("q m j -> q (m j)"),
                         )
 
             return quantise
 
         def prepare_d(g):
             raw = raw_tiles[("D", g // 2)]
-            grouped = stage.tile([P, DIM, PACK], BF16, tag="grouped_d", align_bytes=64, bufs=1)
-            nc.vector.tensor_copy(
-                out=grouped[:].rearrange("p (c i) j -> p c j i", i=RUN),
-                in_=raw[:, g % 2].rearrange("p (j c i) -> p c j i", j=PACK, i=RUN),
+            grouped = stage.tile([P, DIM, PACK], BF16, tag="grouped_k", align_bytes=64)
+            copy_out(
+                D_ENGINES[g],
+                grouped[:].rearrange("p (c i) j -> p c j i", i=RUN),
+                raw[:, g % 2].rearrange("p (j c i) -> p c j i", j=PACK, i=RUN),
             )
 
             def quantise():
@@ -207,82 +194,90 @@ def tile_originaltemporalsae_pa_kernel(tc, o, o_w, o_b, D, x, out_0, out_1):
 
             return quantise
 
-        d_tiles = {}
-        r_tiles = {}
+        relu_t = {}
         r_codes = {}
         r_scales = {}
         accs = {}
         dz_tiles = {}
+        z_tiles = {}
 
-        def multiply(i, g, first=0, width=K_PASS):
+        def multiply(q, m0, blocks, tag="mm"):
+            first, tiles = CHUNKS[q]
+            rows = slice(first * P, (first + tiles) * P)
+            acc = psum.tile([P, blocks, tiles * P], F32, tag=tag)
+            accs[(q, m0)] = acc
+            for k in range(blocks):
+                for c in range(PASSES):
+                    nc.tensor.matmul_mx(
+                        out=acc[:, k],
+                        lhsT=w_codes[:, m0 + k, c].bitcast(FP8X4),
+                        lhsT_scale=w_scales[:, m0 + k, c],
+                        rhs=o_codes[:, c, rows].bitcast(FP8X4),
+                        rhs_scale=o_scales[:, c, rows],
+                        start=(c == 0),
+                        stop=(c == PASSES - 1),
+                    )
+
+        def relu(q, m0, blocks, engine="S"):
+            tiles = CHUNKS[q][1]
+            for k in range(blocks):
+                g, j = (m0 + k) // PACK, (m0 + k) % PACK
+                if j == 0 and q < 3:
+                    width = (4 * P, 2 * P, 2 * P)[q]
+                    if q < 2:
+                        r_tile = relu_pool.tile([P, PACK, width], F32, tag="relu%d" % q)
+                    else:
+                        r_tile = raw_pool.tile([P, PACK, width], F32, tag="raw")
+                    relu_t[(q, g)] = r_tile[:]
+                    if q == 2:
+                        relu_t[(q, g)] = r_tile[:, :, 0:P]
+                        relu_t[(q + 1, g)] = r_tile[:, :, P : 2 * P]
+                out = relu_t[(q, g)][:, j]
+                in_ = accs[(q, m0)][:, k]
+                one = bias[:, m0 + k : m0 + k + 1]
+                if engine == "S":
+                    nc.scalar.activation(out=out, in_=in_, func=ACT.Relu, bias=one)
+                else:
+                    nc.vector.tensor_scalar(
+                        out=out, in0=in_, scalar1=one, scalar2=0.0, op0=ALU.add, op1=ALU.max
+                    )
+
+        def regroup(q, g):
+            rows = CHUNKS[q][1] * P
             if g == 0:
-                d_tile = d_pool.tile([P, WIDTH], F32, tag="d")
-                d_tiles[i] = d_tile
-            cols = slice(g * K_PASS + first, g * K_PASS + first + width)
-            acc = psum.tile([P, width], F32, tag="mm", bufs=4)
-            accs[(i, g, first)] = acc
-            for c in range(PASSES):
-                nc.tensor.matmul_mx(
-                    out=acc[:],
-                    lhsT=o_codes[:, i, c].bitcast(FP8X4),
-                    lhsT_scale=o_scales[:, i, c],
-                    rhs=w_codes[:, c, cols].bitcast(FP8X4),
-                    rhs_scale=w_scales[:, c, cols],
-                    start=(c == 0),
-                    stop=(c == PASSES - 1),
-                )
-
-        def add_bias(i, g, first=0, width=K_PASS):
-            cols = slice(g * K_PASS + first, g * K_PASS + first + width)
-            nc.vector.tensor_tensor(
-                out=d_tiles[i][:, cols], in0=accs[(i, g, first)][:], in1=bias[:, cols], op=ALU.add
+                codes = const.tile([P, GROUPS, rows], U32, tag="r_codes%d" % q, align_bytes=64)
+                scales = const.tile([P, GROUPS, rows], U8, tag="r_scales%d" % q, align_bytes=64)
+                r_codes[q] = codes
+                r_scales[q] = scales
+            grouped = stage.tile([P, rows, PACK], BF16, tag="grouped_k", align_bytes=64)
+            nc.vector.tensor_copy(
+                out=grouped[:].rearrange("p (c i) j -> p c j i", i=RUN),
+                in_=relu_t[(q, g)].rearrange("p j (c i) -> p c j i", i=RUN),
             )
-
-        def relu(i, g, first=0, width=K_PASS):
-            cols = slice(g * K_PASS + first, g * K_PASS + first + width)
-            pairs = slice(first // PACK, (first + width) // PACK)
-            if g % 2 == 0:
-                r_tile = stage.tile([P, 2, 2, P, 2], BF16, tag="r_bf", bufs=7)
-                r_tiles[(i, g // 2)] = r_tile
-            nc.scalar.activation(
-                out=r_tiles[(i, g // 2)][:, g % 2, :, pairs],
-                in_=d_tiles[i][:, cols].rearrange("r (w u e) -> r u w e", u=2, e=2),
-                func=ACT.Relu,
-            )
-
-        def turn_r(i, h, places=(0, 1)):
-            words = r_tiles[(i, h)][:].rearrange("r s u w e -> r (s u w e)").bitcast(F32)
-            bank = psum.tile([P, len(places), 2, P], F32, tag="tp", bufs=4)
-            for k, s in enumerate(places):
-                for u in range(2):
-                    first = (s * 2 + u) * P
-                    nc.tensor.transpose(bank[:, k, u], words[:, first : first + P], ident[:])
-            grouped = stage.tile([P, len(places), P, PACK], BF16, tag="grouped_r", align_bytes=64)
-            copy_out("S", grouped[:].bitcast(F32), bank[:].rearrange("q s u m -> q s m u"))
-            groups = slice(2 * h + places[0], 2 * h + places[-1] + 1)
-            if h == 0:
-                codes = stage.tile([P, GROUPS, P], U32, tag="r_codes", align_bytes=64, bufs=5)
-                scales = stage.tile([P, GROUPS, P], U8, tag="r_scales", align_bytes=64, bufs=5)
-                r_codes[i] = codes
-                r_scales[i] = scales
 
             def quantise():
                 nc.vector.quantize_mx(
-                    out=r_codes[i][:, groups].rearrange("p g m -> p (g m)").bitcast(FP8X4),
-                    scales=r_scales[i][:, groups].rearrange("p g m -> p (g m)"),
-                    in_=grouped[:].rearrange("q g m t -> q (g m t)"),
+                    out=r_codes[q][:, g].bitcast(FP8X4),
+                    scales=r_scales[q][:, g],
+                    in_=grouped[:].rearrange("p r j -> p (r j)"),
                 )
 
             return quantise
 
+        chunk_of = {}
+        for q, (first, tiles) in enumerate(CHUNKS):
+            for t in range(tiles):
+                chunk_of[first + t] = (q, slice(t * P, (t + 1) * P))
+
         def second(i):
-            dz = psum.tile([P, DIM], F32, tag="mm", bufs=4)
+            q, here = chunk_of[i]
+            dz = psum.tile([P, DIM], F32, tag="mm")
             dz_tiles[i] = dz
             for g in range(GROUPS):
                 nc.tensor.matmul_mx(
                     out=dz[:],
-                    lhsT=r_codes[i][:, g].bitcast(FP8X4),
-                    lhsT_scale=r_scales[i][:, g],
+                    lhsT=r_codes[q][:, g, here].bitcast(FP8X4),
+                    lhsT_scale=r_scales[q][:, g, here],
                     rhs=d_codes[:, g].bitcast(FP8X4),
                     rhs_scale=d_scales[:, g],
                     start=(g == 0),
@@ -318,149 +313,165 @@ def tile_originaltemporalsae_pa_kernel(tc, o, o_w, o_b, D, x, out_0, out_1):
             nc.vector.tensor_tensor(out=proj[:, one], in0=dot[:, one], in1=inv[:, one], op=ALU.mult)
 
         def make_x_pred(i):
-            one = slice(i, i + 1)
-            rows = slice(i * P, (i + 1) * P)
             x_pred = stage.tile([P, DIM], F32, tag="x_pred")
-            nc.scalar.activation(out=x_pred[:], in_=dz_tiles[i][:], func=ACT.Copy, scale=proj[:, one])
-            nc.sync.dma_start(out=xp_rows[rows, :], in_=x_pred[:])
-
-        def make_z(i, h):
-            rows = slice(i * P, (i + 1) * P)
-            cols = slice(h * WIDTH // 2, (h + 1) * WIDTH // 2)
-            nc.vector.tensor_scalar(
-                out=d_tiles[i][:, cols],
-                in0=d_tiles[i][:, cols],
-                scalar1=0.0,
-                scalar2=proj[:, i : i + 1],
-                op0=ALU.max,
-                op1=ALU.mult,
+            nc.scalar.activation(
+                out=x_pred[:], in_=dz_tiles[i][:], func=ACT.Copy, scale=proj[:, i : i + 1]
             )
-            nc.sync.dma_start(out=z_rows[rows, cols], in_=d_tiles[i][:, cols])
+            nc.sync.dma_start(out=xp_rows[i * P : (i + 1) * P, :], in_=x_pred[:])
 
-        bias_row = stage.tile([P, WIDTH], BF16, tag="words", bufs=4)
-        nc.vector.memset(ones[:], 1.0)
+        def turn_z(i, g):
+            q, here = chunk_of[i]
+            bank = psum.tile([P, PACK, P], F32, tag="tp")
+            for j in range(PACK):
+                nc.tensor.transpose(bank[:, j], relu_t[(q, g)][:, j, here], ident[:])
+            return bank[:].rearrange("r j p -> r p j")
+
+        def make_z(i, g, turned, engine):
+            if g % 2 == 0:
+                z_sb = stage.tile([P, 2, P, PACK], F32, tag="z_sb", bufs=3)
+                z_tiles[(i, g // 2)] = z_sb
+            z_sb = z_tiles[(i, g // 2)]
+            one = proj[:, i : i + 1]
+            if engine == "S":
+                nc.scalar.activation(out=z_sb[:, g % 2], in_=turned, func=ACT.Copy, scale=one)
+            else:
+                nc.vector.tensor_scalar(
+                    out=z_sb[:, g % 2], in0=turned, scalar1=one, scalar2=None, op0=ALU.mult
+                )
+            if g % 2 == 1:
+                nc.sync.dma_start(
+                    out=z_rows[i * P : (i + 1) * P, (g - 1) * K_PASS : (g + 1) * K_PASS],
+                    in_=z_sb[:].rearrange("r s p j -> r (s p j)"),
+                )
+
         nc.vector.memset(zeros[:], 0.0)
-        nc.vector.memset(bias_row[:], 0.0)
         nc.vector.memset(eps[:], EPS)
         nc.scalar.activation(out=warm[:], in_=eps[:], func=ACT.Sqrt)
-        load_next()
-        nc.sync.dma_start(out=bias_row[0:1, :], in_=o_b.rearrange("(a k) -> a k", a=1))
-        for k in range(RAW_BUFS - 1):
+        for k in range(RAW_BUFS):
             load_next()
+        nc.scalar.dma_start(out=bias_raw[:], in_=o_b.rearrange("(g p j) -> p g j", p=P, j=PACK))
         make_identity(nc, ident[:])
 
-        def keep_warm(count):
-            idle = psum.tile([P, K_PASS], F32, tag="mm", bufs=4)
-            for k in range(count):
-                nc.tensor.matmul(idle[:], lhsT=ones[:], rhs=zeros[:], start=True, stop=True)
-
-        def spread_bias(g):
-            cols = slice(g * K_PASS, (g + 1) * K_PASS)
-            bank = psum.tile([P, K_PASS], F32, tag="mm", bufs=4)
-            nc.tensor.matmul(bank[:], lhsT=ones[:], rhs=bias_row[:, cols], start=True, stop=True)
-            copy_out("SV"[g % 2], bias[:, cols], bank[:])
-
-        def sort_engine(key):
-            return SORT_O if key[0] == "o" else SORT_W[key[2]]
-
-        def is_sorted(n):
-            return n in turn_at and (turn_at[n][0] == "o" and turn_at[n][1] >= 4 or n >= FIRST_SORT and turn_at[n][0] == "w" and n % 4 in SORT_SET)
+        def is_sorted(n, key):
+            return n >= FIRST_SORT and not (key[0] == "w" and key[1] % 4 in NO_SORT)
 
         used = {}
+        sort_at = {}
         for n in turn_at:
-            key = turn_at[n]
-            raw = ("o", key[1] // 2) if key[0] == "o" else key[:2]
-            last_use = n - LEAD if is_sorted(n) else n
-            used[raw] = max(used.get(raw, 0), last_use)
+            for key in turn_at[n]:
+                raw = (key[0], key[1] // 2)
+                use = n
+                if is_sorted(n, key):
+                    use = n - (O_SORT if key[0] == "o" and key[1] >= 6 else LEAD)
+                    sort_at.setdefault(use, []).append(key)
+                used[raw] = max(used.get(raw, 0), use)
         for g in range(GROUPS):
-            used[("D", g // 2)] = D_FIRST + D_STEP * (g // 2 * 2 + 1)
+            used[("D", g // 2)] = D_AT[g // 2 * 2 + 1]
 
-        ready_first = min(multiply_at)
+        def keep_warm(count):
+            idle = psum.tile([P, K_PASS], F32, tag="mm")
+            for k in range(count):
+                nc.tensor.matmul(idle[:], lhsT=zeros[:, 0:P], rhs=zeros[:], start=True, stop=True)
+
         keep_warm(4)
-        d_ready = []
+        late = []
         for n in range(steps):
-            before = multiply_at.get(n - 1)
-            second_before = second_at.get(n - 1)
+            before = second_at.get(n - 1)
             quantises = []
-            if second_before is not None:
-                norms(second_before)
-            if is_sorted(n + LEAD):
-                sort_words(turn_at[n + LEAD], sort_engine(turn_at[n + LEAD]))
-            if n in turn_at:
-                quantises.append(prepare(turn_at[n]))
-            for i, h in turn_r_at.get(n, []):
-                quantises.append(turn_r(i, h))
-            if 2 <= n < 2 + GROUPS:
-                spread_bias(n - 2)
-            if n < ready_first - 1:
-                keep_warm(1)
+            if before is not None:
+                norms(before)
+            for key in sort_at.get(n, []):
+                sort_words(key)
+            for key in turn_at.get(n, []):
+                quantises.append(prepare(key))
+            for i, g in z_at.get(n, []):
+                make_z(i, g, turn_z(i, g), "SV"[g % 2])
             if n in second_at:
                 second(second_at[n])
-            if n in multiply_at:
-                multiply(multiply_at[n][0], multiply_at[n][1])
+            if n in unit_at:
+                multiply(*unit_at[n])
+            if n in WARM:
+                keep_warm(1)
+            if n == 4:
+                nc.vector.tensor_copy(out=bias[:], in_=bias_raw[:].rearrange("p g j -> p (g j)"))
+            if n - 1 in unit_at:
+                relu(*unit_at[n - 1])
             if before is not None:
-                add_bias(before[0], before[1])
-                relu(before[0], before[1])
-            if second_before is not None:
-                product(second_before)
-                project(second_before)
-                make_x_pred(second_before)
+                product(before)
+                project(before)
+                make_x_pred(before)
             if n in second_at:
                 square(second_at[n])
-            for quantise in d_ready + quantises:
+            for quantise in late + quantises:
                 quantise()
-            d_ready = []
-            if second_before is not None:
-                make_z(second_before, 0)
-            if n - 2 in second_at:
-                make_z(second_at[n - 2], 1)
-            if n >= D_FIRST and (n - D_FIRST) % D_STEP == 0 and (n - D_FIRST) // D_STEP < GROUPS:
-                d_ready.append(prepare_d((n - D_FIRST) // D_STEP))
+            late = []
+            for q, g in regroup_at.get(n, []):
+                late.append(regroup(q, g))
+            for g in range(GROUPS):
+                if D_AT[g] == n:
+                    late.append(prepare_d(g))
             for raw in load_order:
                 if used[raw] == n:
                     load_next()
-            if n == D_FIRST + 2:
+            if n == 20:
                 nc.sync.dma_start(out=x_sb[:], in_=x_rows.rearrange("(t p) n -> p t n", p=P))
 
-        i = TILES - 1
-        half = K_PASS // 2
-        quantise_a = turn_r(i, 0)
-        multiply(i, 3, 0, half)
-        multiply(i, 3, half, half)
-        add_bias(i, 2)
-        relu(i, 2)
-        add_bias(i, 3, 0, half)
-        relu(i, 3, 0, half)
-        add_bias(i, 3, half, half)
-        relu(i, 3, half, half)
-        norms(i - 1)
-        quantise_a()
-        product(i - 1)
-        project(i - 1)
-        quantise_b = turn_r(i, 1, (0,))
-        quantise_c = turn_r(i, 1, (1,))
-        quantise_b()
+        last = TILES - 1
+        q = len(CHUNKS) - 1
+        half = DIM // 2
+
+        def turn_and_make_z(i, g):
+            make_z(i, g, turn_z(i, g), "SV"[g % 2])
+
+        turn_and_make_z(last - 2, 0)
+        turn_and_make_z(last - 2, 1)
+        second(last - 1)
+        multiply(q, BLOCKS - 4, 2, "tp")
+        multiply(q, BLOCKS - 2, 2, "tp")
+        relu(*unit_at[steps - 1])
+        square(last - 1)
+        for quantise in late:
+            quantise()
+        quantise_1 = regroup(q, 1)
+        product(last - 1)
+        quantise_1()
+        quantise_2 = regroup(q, 2)
+        norms(last - 1)
+        turn_and_make_z(last - 2, 2)
+        relu(q, BLOCKS - 4, 2, "S")
+        quantise_2()
+        relu(q, BLOCKS - 2, 2, "V")
+        project(last - 1)
+        make_x_pred(last - 1)
+        quantise_3 = regroup(q, 3)
+        turn_and_make_z(last - 2, 3)
+        quantise_3()
         dz_halves = []
         for k in range(2):
-            dz_half = psum.tile([P, half], F32, tag="tp", bufs=4)
+            dz_half = psum.tile([P, half], F32, tag="mm")
             dz_halves.append(dz_half)
-        for g in range(GROUPS):
-            if g == GROUPS - 1:
-                quantise_c()
-            for k in range(2):
-                cols = slice(k * half, (k + 1) * half)
-                nc.tensor.matmul_mx(
-                    out=dz_halves[k][:],
-                    lhsT=r_codes[i][:, g].bitcast(FP8X4),
-                    lhsT_scale=r_scales[i][:, g],
-                    rhs=d_codes[:, g, cols].bitcast(FP8X4),
-                    rhs_scale=d_scales[:, g, cols],
-                    start=(g == 0),
-                    stop=(g == GROUPS - 1),
-                )
-        make_x_pred(i - 1)
-        make_z(i - 1, 0)
-        make_z(i - 1, 1)
+
+        def second_half(g, k):
+            cols = slice(k * half, (k + 1) * half)
+            nc.tensor.matmul_mx(
+                out=dz_halves[k][:],
+                lhsT=r_codes[q][:, g].bitcast(FP8X4),
+                lhsT_scale=r_scales[q][:, g],
+                rhs=d_codes[:, g, cols].bitcast(FP8X4),
+                rhs_scale=d_scales[:, g, cols],
+                start=(g == 0),
+                stop=(g == GROUPS - 1),
+            )
+
+        for g in range(GROUPS - 1):
+            second_half(g, 0)
+            second_half(g, 1)
+        for g in range(2):
+            turn_and_make_z(last - 1, g)
+        second_half(GROUPS - 1, 0)
+        second_half(GROUPS - 1, 1)
+        for g in range(2, GROUPS):
+            turn_and_make_z(last - 1, g)
         sum_sq_half = const.tile([P, 2], F32)
         dot_half = const.tile([P, 2], F32)
         squared = stage.tile([P, DIM], F32, tag="squared", bufs=1)
@@ -476,36 +487,27 @@ def tile_originaltemporalsae_pa_kernel(tc, o, o_w, o_b, D, x, out_0, out_1):
                 out=multiplied[:, k * half : (k + 1) * half],
                 in0=dz_halves[1 - k][:],
                 scalar=1.0,
-                in1=x_sb[:, i, (1 - k) * half : (2 - k) * half],
+                in1=x_sb[:, last, (1 - k) * half : (2 - k) * half],
                 op0=ALU.mult,
                 op1=ALU.mult,
                 accum_out=dot_half[:, k : k + 1],
             )
-        one = slice(i, i + 1)
-        rows = slice(i * P, (i + 1) * P)
+        one = slice(last, last + 1)
+        rows = slice(last * P, (last + 1) * P)
         nc.scalar.activation(
             out=norm[:, one], in_=sum_sq_half[:, 0:1], func=ACT.Sqrt, bias=sum_sq_half[:, 1:2]
         )
         nc.vector.tensor_tensor(out=dot[:, one], in0=dot_half[:, 0:1], in1=dot_half[:, 1:2], op=ALU.add)
         nc.scalar.activation(out=norm_sq[:, one], in_=norm[:, one], func=ACT.Square, bias=eps[:, 0:1])
-        project(i)
+        turned = [turn_z(last, g) for g in range(GROUPS)]
+        project(last)
         x_pred = stage.tile([P, DIM], F32, tag="x_pred")
-        for k in range(2):
-            nc.scalar.activation(
-                out=x_pred[:, k * half : (k + 1) * half],
-                in_=dz_halves[k][:],
-                func=ACT.Copy,
-                scale=proj[:, one],
-            )
-        for k in range(GROUPS):
-            cols = slice(k * K_PASS, (k + 1) * K_PASS)
-            nc.vector.tensor_scalar(
-                out=d_tiles[i][:, cols],
-                in0=d_tiles[i][:, cols],
-                scalar1=0.0,
-                scalar2=proj[:, one],
-                op0=ALU.max,
-                op1=ALU.mult,
-            )
-            nc.sync.dma_start(out=z_rows[rows, cols], in_=d_tiles[i][:, cols])
+        nc.scalar.activation(
+            out=x_pred[:, 0:half], in_=dz_halves[0][:], func=ACT.Copy, scale=proj[:, one]
+        )
+        nc.vector.tensor_scalar(
+            out=x_pred[:, half:DIM], in0=dz_halves[1][:], scalar1=proj[:, one], scalar2=None, op0=ALU.mult
+        )
         nc.sync.dma_start(out=xp_rows[rows, :], in_=x_pred[:])
+        for g in range(GROUPS):
+            make_z(last, g, turned[g], "SV"[g % 2])

@@ -28,15 +28,16 @@ CHUNKS = ((0, 4), (4, 2), (6, 1), (7, 1))
 LEAD = 2
 O_SORT = 5
 LAG = 2
-O_FIRST = 3
-FIRST_SORT = 5
+PAIR_FROM = 8
+O_FIRST = (4, 3, 3)
+FIRST_SORT = 4
 NO_SORT = ()
-D_AT = (18, 20, 21, 22)
+D_AT = (19, 21, 22, 23)
 D_ENGINES = "VSVS"
-S2_FIRST = 27
-S2_NUM = 5
+S2_FIRST = 28
+RG_LAG = (2, 2, 1, 1)
 Z_LAG = 2
-WARM = (0, 1, 2, 3, 4, 5)
+WARM = ()
 
 FLOPS = 2 * ROWS * WIDTH * WIDTH + 2 * ROWS * WIDTH * DIM
 
@@ -62,31 +63,39 @@ def tile_originaltemporalsae_pa_kernel(tc, o, o_w, o_b, D, x, out_0, out_1):
     second_at = {}
     z_at = {}
     early = CHUNKS[0][1]
-    order = [("o", i) for i in range(early)] + [("w", m) for m in range(BLOCKS)]
+    order = [("o", 0), ("o", 1)] + [("w", m) for m in range(4)] + [("o", 2), ("o", 3)]
+    order += [("w", m) for m in range(4, BLOCKS)]
     for n, key in enumerate(order):
-        turn_at.setdefault(n, []).append(key)
-    n = early + LAG
+        turn_at.setdefault(n - n % 2 if n >= PAIR_FROM else n, []).append(key)
+    n = order.index(("w", 0)) + LAG
+    for m in range(4):
+        unit_at[n + m] = (0, m, 1, 0, 2)
+    n = order.index(("o", 3)) + LAG
+    for m in range(0, 4, 2):
+        unit_at[n] = (0, m, 2, 2, 2)
+        unit_step[(0, m + 1)] = n
+        n += 1
     for q, (first, tiles) in enumerate(CHUNKS):
         blocks = early // tiles
         if q > 0:
             for t in range(tiles):
-                turn_at.setdefault(n - O_FIRST + t, []).append(("o", first + t))
-        for m in range(0, BLOCKS, blocks):
-            unit_at[n] = (q, m, blocks)
+                turn_at.setdefault(n - O_FIRST[q - 1] + t, []).append(("o", first + t))
+        for m in range(4 if q == 0 else 0, BLOCKS, blocks):
+            unit_at[n] = (q, m, blocks, first, tiles)
             unit_step[(q, m + blocks - 1)] = n
             n += 1
     for i in range(TILES - 1):
-        second_at[S2_FIRST + S2_NUM * i // 3] = i
+        second_at[S2_FIRST + 3 * i // 2] = i
     for n in second_at:
         for g in range(GROUPS):
-            z_at.setdefault(n + Z_LAG + g // 2, []).append((second_at[n], g))
+            z_at.setdefault(n + Z_LAG, []).append((second_at[n], g))
     regroup_at = {}
     for q in range(len(CHUNKS)):
         for g in range(GROUPS):
-            regroup_at.setdefault(unit_step[(q, PACK * g + PACK - 1)] + 2, []).append((q, g))
+            regroup_at.setdefault(unit_step[(q, PACK * g + PACK - 1)] + RG_LAG[q], []).append((q, g))
     steps = max(unit_at)
 
-    load_order = [("o", 0), ("o", 1)] + [("w", a) for a in range(BLOCKS // 2)]
+    load_order = [("o", 0), ("w", 0), ("w", 1), ("o", 1)] + [("w", a) for a in range(2, BLOCKS // 2)]
     load_order += [("o", 2), ("o", 3), ("D", 0), ("D", 1)]
 
     with ExitStack() as ctx:
@@ -201,11 +210,10 @@ def tile_originaltemporalsae_pa_kernel(tc, o, o_w, o_b, D, x, out_0, out_1):
         dz_tiles = {}
         z_tiles = {}
 
-        def multiply(q, m0, blocks, tag="mm"):
-            first, tiles = CHUNKS[q]
+        def multiply(q, m0, blocks, first, tiles, tag="mm"):
             rows = slice(first * P, (first + tiles) * P)
             acc = psum.tile([P, blocks, tiles * P], F32, tag=tag)
-            accs[(q, m0)] = acc
+            accs[(m0, first)] = acc
             for k in range(blocks):
                 for c in range(PASSES):
                     nc.tensor.matmul_mx(
@@ -218,11 +226,11 @@ def tile_originaltemporalsae_pa_kernel(tc, o, o_w, o_b, D, x, out_0, out_1):
                         stop=(c == PASSES - 1),
                     )
 
-        def relu(q, m0, blocks, engine="S"):
-            tiles = CHUNKS[q][1]
+        def relu(q, m0, blocks, first, tiles, engine="S"):
+            start = (first - CHUNKS[q][0]) * P
             for k in range(blocks):
                 g, j = (m0 + k) // PACK, (m0 + k) % PACK
-                if j == 0 and q < 3:
+                if j == 0 and q < 3 and start == 0:
                     width = (4 * P, 2 * P, 2 * P)[q]
                     if q < 2:
                         r_tile = relu_pool.tile([P, PACK, width], F32, tag="relu%d" % q)
@@ -232,8 +240,8 @@ def tile_originaltemporalsae_pa_kernel(tc, o, o_w, o_b, D, x, out_0, out_1):
                     if q == 2:
                         relu_t[(q, g)] = r_tile[:, :, 0:P]
                         relu_t[(q + 1, g)] = r_tile[:, :, P : 2 * P]
-                out = relu_t[(q, g)][:, j]
-                in_ = accs[(q, m0)][:, k]
+                out = relu_t[(q, g)][:, j, start : start + tiles * P]
+                in_ = accs[(m0, first)][:, k]
                 one = bias[:, m0 + k : m0 + k + 1]
                 if engine == "S":
                     nc.scalar.activation(out=out, in_=in_, func=ACT.Relu, bias=one)
@@ -338,7 +346,12 @@ def tile_originaltemporalsae_pa_kernel(tc, o, o_w, o_b, D, x, out_0, out_1):
                 nc.vector.tensor_scalar(
                     out=z_sb[:, g % 2], in0=turned, scalar1=one, scalar2=None, op0=ALU.mult
                 )
-            if g % 2 == 1:
+            if i == TILES - 1:
+                nc.sync.dma_start(
+                    out=z_rows[i * P : (i + 1) * P, g * K_PASS : (g + 1) * K_PASS],
+                    in_=z_sb[:, g % 2].rearrange("r p j -> r (p j)"),
+                )
+            elif g % 2 == 1:
                 nc.sync.dma_start(
                     out=z_rows[i * P : (i + 1) * P, (g - 1) * K_PASS : (g + 1) * K_PASS],
                     in_=z_sb[:].rearrange("r s p j -> r (s p j)"),
@@ -423,28 +436,20 @@ def tile_originaltemporalsae_pa_kernel(tc, o, o_w, o_b, D, x, out_0, out_1):
         def turn_and_make_z(i, g):
             make_z(i, g, turn_z(i, g), "SV"[g % 2])
 
-        turn_and_make_z(last - 2, 0)
-        turn_and_make_z(last - 2, 1)
-        second(last - 1)
-        multiply(q, BLOCKS - 4, 2, "tp")
-        multiply(q, BLOCKS - 2, 2, "tp")
+        multiply(q, BLOCKS - 4, 2, last, 1, "tp")
+        multiply(q, BLOCKS - 2, 2, last, 1, "tp")
+        norms(last - 1)
         relu(*unit_at[steps - 1])
-        square(last - 1)
         for quantise in late:
             quantise()
-        quantise_1 = regroup(q, 1)
         product(last - 1)
-        quantise_1()
-        quantise_2 = regroup(q, 2)
-        norms(last - 1)
-        turn_and_make_z(last - 2, 2)
-        relu(q, BLOCKS - 4, 2, "S")
-        quantise_2()
-        relu(q, BLOCKS - 2, 2, "V")
         project(last - 1)
-        make_x_pred(last - 1)
+        quantise_2 = regroup(q, 2)
+        relu(q, BLOCKS - 4, 2, last, 1, "S")
+        relu(q, BLOCKS - 2, 2, last, 1, "S")
+        quantise_2()
         quantise_3 = regroup(q, 3)
-        turn_and_make_z(last - 2, 3)
+        make_x_pred(last - 1)
         quantise_3()
         dz_halves = []
         for k in range(2):
@@ -463,15 +468,11 @@ def tile_originaltemporalsae_pa_kernel(tc, o, o_w, o_b, D, x, out_0, out_1):
                 stop=(g == GROUPS - 1),
             )
 
-        for g in range(GROUPS - 1):
+        for g in range(GROUPS):
+            turn_and_make_z(last - 1, g)
+        for g in range(GROUPS):
             second_half(g, 0)
             second_half(g, 1)
-        for g in range(2):
-            turn_and_make_z(last - 1, g)
-        second_half(GROUPS - 1, 0)
-        second_half(GROUPS - 1, 1)
-        for g in range(2, GROUPS):
-            turn_and_make_z(last - 1, g)
         sum_sq_half = const.tile([P, 2], F32)
         dot_half = const.tile([P, 2], F32)
         squared = stage.tile([P, DIM], F32, tag="squared", bufs=1)

@@ -28,7 +28,6 @@ CHUNKS = ((0, 4), (4, 2), (6, 1), (7, 1))
 LEAD = 2
 O_SORT = 5
 LAG = 2
-PAIR_FROM = 8
 O_FIRST = (4, 3, 3)
 FIRST_SORT = 4
 NO_SORT = ()
@@ -66,7 +65,7 @@ def tile_originaltemporalsae_pa_kernel(tc, o, o_w, o_b, D, x, out_0, out_1):
     order = [("o", 0), ("o", 1)] + [("w", m) for m in range(4)] + [("o", 2), ("o", 3)]
     order += [("w", m) for m in range(4, BLOCKS)]
     for n, key in enumerate(order):
-        turn_at.setdefault(n - n % 2 if n >= PAIR_FROM else n, []).append(key)
+        turn_at.setdefault(n, []).append(key)
     n = order.index(("w", 0)) + LAG
     for m in range(4):
         unit_at[n + m] = (0, m, 1, 0, 2)

from contextlib import ExitStack

import concourse.mybir as mybir
from concourse.masks import make_identity

F32 = mybir.dt.float32
BF16 = mybir.dt.bfloat16
U32 = mybir.dt.uint32
U8 = mybir.dt.uint8
FP8X4 = mybir.dt.float8_e4m3fn_x4
ACT = mybir.ActivationFunctionType
ALU = mybir.AluOpType

P = 128
PACK = 4
K_PASS = P * PACK
ROWS = 1024
TILES = ROWS // P
WIDTH = 2048
DIM = 512
PASSES = WIDTH // K_PASS
GROUPS = WIDTH // K_PASS
BLOCKS = WIDTH // P
EPS = 1e-6
RAW_BUFS = 4
RUN = 4
CHUNKS = ((0, 4), (4, 2), (6, 1), (7, 1))
LEAD = 2
O_SORT = 5
LAG = 2
O_FIRST = (4, 3, 3)
FIRST_SORT = 4
NO_SORT = ()
D_AT = (19, 21, 22, 23)
D_ENGINES = "VSVS"
S2_FIRST = 28
RG_LAG = (2, 2, 1, 1)
Z_LAG = 2
WARM = ()

FLOPS = 2 * ROWS * WIDTH * WIDTH + 2 * ROWS * WIDTH * DIM


def tile_originaltemporalsae_pa_kernel(tc, o, o_w, o_b, D, x, out_0, out_1):
    nc = tc.nc
    o_rows = o.flatten_outer_dims()
    x_rows = x.flatten_outer_dims()
    z_rows = out_0.flatten_outer_dims()
    xp_rows = out_1.flatten_outer_dims()

    views = {}
    for a in range(TILES // 2):
        views[("o", a)] = o_rows.rearrange("(a t p) k -> a p t k", t=2, p=P)[a]
    for a in range(BLOCKS // 2):
        views[("w", a)] = o_w.rearrange("(a p h t) k -> a h p t k", p=P, h=2, t=2)[a // 2, a % 2]
    for a in range(GROUPS // 2):
        views[("D", a)] = D.rearrange("(a g p j) n -> a p g (j n)", g=2, p=P, j=PACK)[a]

    turn_at = {}
    unit_at = {}
    unit_step = {}
    second_at = {}
    z_at = {}
    early = CHUNKS[0][1]
    order = [("o", 0), ("o", 1)] + [("w", m) for m in range(4)] + [("o", 2), ("o", 3)]
    order += [("w", m) for m in range(4, BLOCKS)]
    for n, key in enumerate(order):
        turn_at.setdefault(n, []).append(key)
    n = order.index(("w", 0)) + LAG
    for m in range(4):
        unit_at[n + m] = (0, m, 1, 0, 2)
    n = order.index(("o", 3)) + LAG
    for m in range(0, 4, 2):
        unit_at[n] = (0, m, 2, 2, 2)
        unit_step[(0, m + 1)] = n
        n += 1
    for q, (first, tiles) in enumerate(CHUNKS):
        blocks = early // tiles
        if q > 0:
            for t in range(tiles):
                turn_at.setdefault(n - O_FIRST[q - 1] + t, []).append(("o", first + t))
        for m in range(4 if q == 0 else 0, BLOCKS, blocks):
            unit_at[n] = (q, m, blocks, first, tiles)
            unit_step[(q, m + blocks - 1)] = n
            n += 1
    for i in range(TILES - 1):
        second_at[S2_FIRST + 3 * i // 2] = i
    for n in second_at:
        for g in range(GROUPS):
            z_at.setdefault(n + Z_LAG, []).append((second_at[n], g))
    regroup_at = {}
    for q in range(len(CHUNKS)):
        for g in range(GROUPS):
            regroup_at.setdefault(unit_step[(q, PACK * g + PACK - 1)] + RG_LAG[q], []).append((q, g))
    steps = max(unit_at)

    load_order = [("o", 0), ("w", 0), ("w", 1), ("o", 1)] + [("w", a) for a in range(2, BLOCKS // 2)]
    load_order += [("o", 2), ("o", 3), ("D", 0), ("D", 1)]

    with ExitStack() as ctx:
        const = ctx.enter_context(tc.tile_pool(name="const", bufs=1))
        raw_pool = ctx.enter_context(tc.tile_pool(name="raw", bufs=RAW_BUFS))
        stage = ctx.enter_context(tc.tile_pool(name="stage", bufs=2))
        relu_pool = ctx.enter_context(tc.tile_pool(name="relu", bufs=GROUPS))
        psum = ctx.enter_context(tc.psum_pool(name="psum", bufs=4))
        ctx.enter_context(tc.manual_schedule())

        w_codes = const.tile([P, BLOCKS, PASSES, P], U32, align_bytes=64)
        w_scales = const.tile([P, BLOCKS, PASSES, P], U8, align_bytes=64)
        o_codes = const.tile([P, PASSES, ROWS], U32, align_bytes=64)
        o_scales = const.tile([P, PASSES, ROWS], U8, align_bytes=64)
        d_codes = const.tile([P, GROUPS, DIM], U32, align_bytes=64)
        d_scales = const.tile([P, GROUPS, DIM], U8, align_bytes=64)
        x_sb = const.tile([P, TILES, DIM], BF16)
        ident = const.tile([P, P], F32)
        bias_raw = const.tile([P, GROUPS, PACK], BF16)
        bias = const.tile([P, BLOCKS], F32)
        eps = const.tile([P, 1], F32)
        zeros = const.tile([P, K_PASS], BF16)
        warm = const.tile([P, 1], F32)
        sum_sq = const.tile([P, TILES], F32)
        norm = const.tile([P, TILES], F32)
        norm_sq = const.tile([P, TILES], F32)
        dot = const.tile([P, TILES], F32)
        inv = const.tile([P, TILES], F32)
        proj = const.tile([P, TILES], F32)

        raw_tiles = {}

        def load_next():
            if len(raw_tiles) < len(load_order):
                key = load_order[len(raw_tiles)]
                raw = raw_pool.tile([P, 2, WIDTH], BF16, tag="raw")
                for t in range(2):
                    nc.sync.dma_start(out=raw[:, t], in_=views[key][:, t])
                raw_tiles[key] = raw

        def copy_out(engine, out, in_):
            if engine == "S":
                nc.scalar.copy(out=out, in_=in_)
            else:
                nc.vector.tensor_copy(out=out, in_=in_)

        def row_words(key):
            return raw_tiles[(key[0], key[1] // 2)][:, key[1] % 2].bitcast(F32)

        sorted_words = {}

        def sort_words(key):
            words = stage.tile([P, 2, WIDTH // 4], F32, tag="words", bufs=4)
            nc.vector.tensor_copy(out=words[:], in_=row_words(key).rearrange("r (w u) -> r u w", u=2))
            sorted_words[key] = words

        def prepare(key):
            grouped = stage.tile([P, PASSES, P, PACK], BF16, tag="grouped", align_bytes=64, bufs=3)
            words = grouped[:].bitcast(F32)
            for b in range(PASSES // 2):
                bank = psum.tile([P, 2, 2, P], F32, tag="tp")
                for s in range(2):
                    c = 2 * b + s
                    for u in range(2):
                        if key in sorted_words:
                            in_ = sorted_words[key][:, u, c * P : (c + 1) * P]
                        else:
                            in_ = row_words(key)[:, 2 * c * P + u : 2 * (c + 1) * P : 2]
                        nc.tensor.transpose(bank[:, s, u], in_, ident[:])
                copy_out("S", words[:, 2 * b : 2 * b + 2], bank[:].rearrange("q s u m -> q s m u"))

            def quantise():
                if key[0] == "w":
                    nc.vector.quantize_mx(
                        out=w_codes[:, key[1]].rearrange("q c m -> q (c m)").bitcast(FP8X4),
                        scales=w_scales[:, key[1]].rearrange("q c m -> q (c m)"),
                        in_=grouped[:].rearrange("q c m j -> q (c m j)"),
                    )
                else:
                    cols = slice(key[1] * P, (key[1] + 1) * P)
                    for c in range(PASSES):
                        nc.vector.quantize_mx(
                            out=o_codes[:, c, cols].bitcast(FP8X4),
                            scales=o_scales[:, c, cols],
                            in_=grouped[:, c].rearrange("q m j -> q (m j)"),
                        )

            return quantise

        def prepare_d(g):
            raw = raw_tiles[("D", g // 2)]
            grouped = stage.tile([P, DIM, PACK], BF16, tag="grouped_k", align_bytes=64)
            copy_out(
                D_ENGINES[g],
                grouped[:].rearrange("p (c i) j -> p c j i", i=RUN),
                raw[:, g % 2].rearrange("p (j c i) -> p c j i", j=PACK, i=RUN),
            )

            def quantise():
                nc.vector.quantize_mx(
                    out=d_codes[:, g].bitcast(FP8X4),
                    scales=d_scales[:, g],
                    in_=grouped[:].rearrange("p n j -> p (n j)"),
                )

            return quantise

        relu_t = {}
        r_codes = {}
        r_scales = {}
        accs = {}
        dz_tiles = {}
        z_tiles = {}

        def multiply(q, m0, blocks, first, tiles, tag="mm"):
            rows = slice(first * P, (first + tiles) * P)
            acc = psum.tile([P, blocks, tiles * P], F32, tag=tag)
            accs[(m0, first)] = acc
            for k in range(blocks):
                for c in range(PASSES):
                    nc.tensor.matmul_mx(
                        out=acc[:, k],
                        lhsT=w_codes[:, m0 + k, c].bitcast(FP8X4),
                        lhsT_scale=w_scales[:, m0 + k, c],
                        rhs=o_codes[:, c, rows].bitcast(FP8X4),
                        rhs_scale=o_scales[:, c, rows],
                        start=(c == 0),
                        stop=(c == PASSES - 1),
                    )

        def relu(q, m0, blocks, first, tiles, engine="S"):
            start = (first - CHUNKS[q][0]) * P
            for k in range(blocks):
                g, j = (m0 + k) // PACK, (m0 + k) % PACK
                if j == 0 and q < 3 and start == 0:
                    width = (4 * P, 2 * P, 2 * P)[q]
                    if q < 2:
                        r_tile = relu_pool.tile([P, PACK, width], F32, tag="relu%d" % q)
                    else:
                        r_tile = raw_pool.tile([P, PACK, width], F32, tag="raw")
                    relu_t[(q, g)] = r_tile[:]
                    if q == 2:
                        relu_t[(q, g)] = r_tile[:, :, 0:P]
                        relu_t[(q + 1, g)] = r_tile[:, :, P : 2 * P]
                out = relu_t[(q, g)][:, j, start : start + tiles * P]
                in_ = accs[(m0, first)][:, k]
                one = bias[:, m0 + k : m0 + k + 1]
                if engine == "S":
                    nc.scalar.activation(out=out, in_=in_, func=ACT.Relu, bias=one)
                else:
                    nc.vector.tensor_scalar(
                        out=out, in0=in_, scalar1=one, scalar2=0.0, op0=ALU.add, op1=ALU.max
                    )

        def regroup(q, g):
            rows = CHUNKS[q][1] * P
            if g == 0:
                codes = const.tile([P, GROUPS, rows], U32, tag="r_codes%d" % q, align_bytes=64)
                scales = const.tile([P, GROUPS, rows], U8, tag="r_scales%d" % q, align_bytes=64)
                r_codes[q] = codes
                r_scales[q] = scales
            grouped = stage.tile([P, rows, PACK], BF16, tag="grouped_k", align_bytes=64)
            nc.vector.tensor_copy(
                out=grouped[:].rearrange("p (c i) j -> p c j i", i=RUN),
                in_=relu_t[(q, g)].rearrange("p j (c i) -> p c j i", i=RUN),
            )

            def quantise():
                nc.vector.quantize_mx(
                    out=r_codes[q][:, g].bitcast(FP8X4),
                    scales=r_scales[q][:, g],
                    in_=grouped[:].rearrange("p r j -> p (r j)"),
                )

            return quantise

        chunk_of = {}
        for q, (first, tiles) in enumerate(CHUNKS):
            for t in range(tiles):
                chunk_of[first + t] = (q, slice(t * P, (t + 1) * P))

        def second(i):
            q, here = chunk_of[i]
            dz = psum.tile([P, DIM], F32, tag="mm")
            dz_tiles[i] = dz
            for g in range(GROUPS):
                nc.tensor.matmul_mx(
                    out=dz[:],
                    lhsT=r_codes[q][:, g, here].bitcast(FP8X4),
                    lhsT_scale=r_scales[q][:, g, here],
                    rhs=d_codes[:, g].bitcast(FP8X4),
                    rhs_scale=d_scales[:, g],
                    start=(g == 0),
                    stop=(g == GROUPS - 1),
                )

        def square(i):
            squared = stage.tile([P, DIM], F32, tag="squared", bufs=1)
            nc.scalar.activation(
                out=squared[:], in_=dz_tiles[i][:], func=ACT.Square, accum_out=sum_sq[:, i : i + 1]
            )

        def product(i):
            multiplied = stage.tile([P, DIM], F32, tag="multiplied", bufs=1)
            nc.vector.scalar_tensor_tensor(
                out=multiplied[:],
                in0=dz_tiles[i][:],
                scalar=1.0,
                in1=x_sb[:, i],
                op0=ALU.mult,
                op1=ALU.mult,
                accum_out=dot[:, i : i + 1],
            )

        def norms(i):
            one = slice(i, i + 1)
            nc.scalar.activation(out=norm[:, one], in_=sum_sq[:, one], func=ACT.Sqrt)
            nc.scalar.activation(out=norm_sq[:, one], in_=norm[:, one], func=ACT.Square, bias=eps[:, 0:1])

        def project(i):
            one = slice(i, i + 1)
            nc.vector.reciprocal(out=inv[:, one], in_=norm_sq[:, one])
            nc.vector.tensor_tensor(out=proj[:, one], in0=dot[:, one], in1=inv[:, one], op=ALU.mult)

        def make_x_pred(i):
            x_pred = stage.tile([P, DIM], F32, tag="x_pred")
            nc.scalar.activation(
                out=x_pred[:], in_=dz_tiles[i][:], func=ACT.Copy, scale=proj[:, i : i + 1]
            )
            nc.sync.dma_start(out=xp_rows[i * P : (i + 1) * P, :], in_=x_pred[:])

        def turn_z(i, g):
            q, here = chunk_of[i]
            bank = psum.tile([P, PACK, P], F32, tag="tp")
            for j in range(PACK):
                nc.tensor.transpose(bank[:, j], relu_t[(q, g)][:, j, here], ident[:])
            return bank[:].rearrange("r j p -> r p j")

        def make_z(i, g, turned, engine):
            if g % 2 == 0:
                z_sb = stage.tile([P, 2, P, PACK], F32, tag="z_sb", bufs=3)
                z_tiles[(i, g // 2)] = z_sb
            z_sb = z_tiles[(i, g // 2)]
            one = proj[:, i : i + 1]
            if engine == "S":
                nc.scalar.activation(out=z_sb[:, g % 2], in_=turned, func=ACT.Copy, scale=one)
            else:
                nc.vector.tensor_scalar(
                    out=z_sb[:, g % 2], in0=turned, scalar1=one, scalar2=None, op0=ALU.mult
                )
            if i == TILES - 1:
                nc.sync.dma_start(
                    out=z_rows[i * P : (i + 1) * P, g * K_PASS : (g + 1) * K_PASS],
                    in_=z_sb[:, g % 2].rearrange("r p j -> r (p j)"),
                )
            elif g % 2 == 1:
                nc.sync.dma_start(
                    out=z_rows[i * P : (i + 1) * P, (g - 1) * K_PASS : (g + 1) * K_PASS],
                    in_=z_sb[:].rearrange("r s p j -> r (s p j)"),
                )

        nc.vector.memset(zeros[:], 0.0)
        nc.vector.memset(eps[:], EPS)
        nc.scalar.activation(out=warm[:], in_=eps[:], func=ACT.Sqrt)
        for k in range(RAW_BUFS):
            load_next()
        nc.scalar.dma_start(out=bias_raw[:], in_=o_b.rearrange("(g p j) -> p g j", p=P, j=PACK))
        make_identity(nc, ident[:])

        def is_sorted(n, key):
            return n >= FIRST_SORT and not (key[0] == "w" and key[1] % 4 in NO_SORT)

        used = {}
        sort_at = {}
        for n in turn_at:
            for key in turn_at[n]:
                raw = (key[0], key[1] // 2)
                use = n
                if is_sorted(n, key):
                    use = n - (O_SORT if key[0] == "o" and key[1] >= 6 else LEAD)
                    sort_at.setdefault(use, []).append(key)
                used[raw] = max(used.get(raw, 0), use)
        for g in range(GROUPS):
            used[("D", g // 2)] = D_AT[g // 2 * 2 + 1]

        def keep_warm(count):
            idle = psum.tile([P, K_PASS], F32, tag="mm")
            for k in range(count):
                nc.tensor.matmul(idle[:], lhsT=zeros[:, 0:P], rhs=zeros[:], start=True, stop=True)

        keep_warm(4)
        late = []
        for n in range(steps):
            before = second_at.get(n - 1)
            quantises = []
            if before is not None:
                norms(before)
            for key in sort_at.get(n, []):
                sort_words(key)
            for key in turn_at.get(n, []):
                quantises.append(prepare(key))
            for i, g in z_at.get(n, []):
                make_z(i, g, turn_z(i, g), "SV"[g % 2])
            if n in second_at:
                second(second_at[n])
            if n in unit_at:
                multiply(*unit_at[n])
            if n in WARM:
                keep_warm(1)
            if n == 4:
                nc.vector.tensor_copy(out=bias[:], in_=bias_raw[:].rearrange("p g j -> p (g j)"))
            if n - 1 in unit_at:
                relu(*unit_at[n - 1])
            if before is not None:
                product(before)
                project(before)
                make_x_pred(before)
            if n in second_at:
                square(second_at[n])
            for quantise in late + quantises:
                quantise()
            late = []
            for q, g in regroup_at.get(n, []):
                late.append(regroup(q, g))
            for g in range(GROUPS):
                if D_AT[g] == n:
                    late.append(prepare_d(g))
            for raw in load_order:
                if used[raw] == n:
                    load_next()
            if n == 20:
                nc.sync.dma_start(out=x_sb[:], in_=x_rows.rearrange("(t p) n -> p t n", p=P))

        last = TILES - 1
        q = len(CHUNKS) - 1
        half = DIM // 2

        def turn_and_make_z(i, g):
            make_z(i, g, turn_z(i, g), "SV"[g % 2])

        multiply(q, BLOCKS - 4, 2, last, 1, "tp")
        multiply(q, BLOCKS - 2, 2, last, 1, "tp")
        norms(last - 1)
        relu(*unit_at[steps - 1])
        for quantise in late:
            quantise()
        product(last - 1)
        project(last - 1)
        quantise_2 = regroup(q, 2)
        relu(q, BLOCKS - 4, 2, last, 1, "S")
        relu(q, BLOCKS - 2, 2, last, 1, "S")
        quantise_2()
        quantise_3 = regroup(q, 3)
        make_x_pred(last - 1)
        quantise_3()
        dz_halves = []
        for k in range(2):
            dz_half = psum.tile([P, half], F32, tag="mm")
            dz_halves.append(dz_half)

        def second_half(g, k):
            cols = slice(k * half, (k + 1) * half)
            nc.tensor.matmul_mx(
                out=dz_halves[k][:],
                lhsT=r_codes[q][:, g].bitcast(FP8X4),
                lhsT_scale=r_scales[q][:, g],
                rhs=d_codes[:, g, cols].bitcast(FP8X4),
                rhs_scale=d_scales[:, g, cols],
                start=(g == 0),
                stop=(g == GROUPS - 1),
            )

        for g in range(GROUPS):
            turn_and_make_z(last - 1, g)
        for g in range(GROUPS):
            second_half(g, 0)
            second_half(g, 1)
        sum_sq_half = const.tile([P, 2], F32)
        dot_half = const.tile([P, 2], F32)
        squared = stage.tile([P, DIM], F32, tag="squared", bufs=1)
        multiplied = stage.tile([P, DIM], F32, tag="multiplied", bufs=1)
        for k in range(2):
            nc.scalar.activation(
                out=squared[:, k * half : (k + 1) * half],
                in_=dz_halves[k][:],
                func=ACT.Square,
                accum_out=sum_sq_half[:, k : k + 1],
            )
            nc.vector.scalar_tensor_tensor(
                out=multiplied[:, k * half : (k + 1) * half],
                in0=dz_halves[1 - k][:],
                scalar=1.0,
                in1=x_sb[:, last, (1 - k) * half : (2 - k) * half],
                op0=ALU.mult,
                op1=ALU.mult,
                accum_out=dot_half[:, k : k + 1],
            )
        one = slice(last, last + 1)
        rows = slice(last * P, (last + 1) * P)
        nc.scalar.activation(
            out=norm[:, one], in_=sum_sq_half[:, 0:1], func=ACT.Sqrt, bias=sum_sq_half[:, 1:2]
        )
        nc.vector.tensor_tensor(out=dot[:, one], in0=dot_half[:, 0:1], in1=dot_half[:, 1:2], op=ALU.add)
        nc.scalar.activation(out=norm_sq[:, one], in_=norm[:, one], func=ACT.Square, bias=eps[:, 0:1])
        turned = [turn_z(last, g) for g in range(GROUPS)]
        project(last)
        x_pred = stage.tile([P, DIM], F32, tag="x_pred")
        nc.scalar.activation(
            out=x_pred[:, 0:half], in_=dz_halves[0][:], func=ACT.Copy, scale=proj[:, one]
        )
        nc.vector.tensor_scalar(
            out=x_pred[:, half:DIM], in0=dz_halves[1][:], scalar1=proj[:, one], scalar2=None, op0=ALU.mult
        )
        nc.sync.dma_start(out=xp_rows[rows, :], in_=x_pred[:])
        for g in range(GROUPS):
            make_z(last, g, turned[g], "SV"[g % 2])
